import numpy as np
import ml_dtypes


def mxq(x, axis, fmt="e4m3"):
    dtype, down = {"e4m3": (ml_dtypes.float8_e4m3fn, 7), "e5m2": (ml_dtypes.float8_e5m2, 14)}[fmt]
    v = np.moveaxis(np.asarray(x, np.float32).astype(ml_dtypes.bfloat16).astype(np.float64), axis, -1)
    blocks = v.reshape(v.shape[:-1] + (-1, 32))
    amax = np.abs(blocks).max(-1, keepdims=True)
    byte = np.maximum(np.where(amax > 0, np.frexp(amax)[1] - 1 + 127, 0) - down, 1)
    scale = np.exp2(byte - 127.0)
    codes = (blocks / scale).astype(np.float32).astype(dtype).astype(np.float64)
    return np.moveaxis((codes * scale).reshape(v.shape), -1, axis)


WIDE = False


def mx_kscale(k):
    if not WIDE:
        return np.ones(k)
    levels = np.array([10, -10, 5, -5, 0])
    a = np.random.permutation(np.resize(levels, k // 512 * 4)).reshape(k // 512, 4)
    idx = np.arange(k)
    return np.exp2(a[idx // 512, idx % 128 // 32])


BF16 = ml_dtypes.bfloat16


def bf(x):
    return np.asarray(x, np.float32).astype(BF16)


def f64(x):
    return np.asarray(x).astype(np.float64)


B, SY, SX, D, F = 2, 512, 2048, 512, 2048
EPS = 1e-5


def layer_norm_all(t):
    mu = t.mean()
    var = np.square(t - mu).mean()
    return (t - mu) / np.sqrt(var + EPS)


def setup_inputs():
    t = mx_kscale(F)
    return {"h2": bf(np.random.standard_normal((B, SY, D))),
            "w_ff1": bf(np.random.standard_normal((F, D)) / np.sqrt(D) * t[:, None]),
            "b_ff1": bf(np.random.standard_normal(F) * 0.3 * t),
            "w_ff2": bf(np.random.standard_normal((D, F)) * 1.4 / np.sqrt(F) / t[None, :]),
            "b_ff2": bf(0.2 + 0.2 * np.random.standard_normal(D))}


def reference(h2, w_ff1, b_ff1, w_ff2, b_ff2):
    h = f64(h2)
    a = np.maximum((mxq(h, 2, "e4m3") @ mxq(f64(w_ff1), 1, "e4m3").T) + f64(b_ff1), 0.0)
    ff = (mxq(a, 2, "e4m3") @ mxq(f64(w_ff2), 1, "e4m3").T) + f64(b_ff2)
    return layer_norm_all(h + ff)

@@ -1,0 +1,374 @@
+from contextlib import ExitStack
+
+import concourse.mybir as mybir
+from concourse.masks import make_identity
+
+F32 = mybir.dt.float32
+BF16 = mybir.dt.bfloat16
+U32 = mybir.dt.uint32
+U8 = mybir.dt.uint8
+FP8X4 = mybir.dt.float8_e4m3fn_x4
+ACT = mybir.ActivationFunctionType
+ALU = mybir.AluOpType
+AXIS = mybir.AxisListType
+
+P = 128
+PACK = 4
+K_PASS = P * PACK
+BANK = 512
+PAIR = 2
+
+TOKENS = 1024
+D = 512
+F = 2048
+EPS = 1e-5
+
+TOKEN_TILES = TOKENS // P
+HALF_TOKENS = TOKENS // 2
+HALF_TILES = HALF_TOKENS // P
+GROUPS = F // K_PASS
+F_TILES = F // P
+D_TILES = D // P
+UNITS = 2 * GROUPS
+LAG = 2
+
+FLOPS = 2 * TOKENS * D * F * 2
+
+
+def tile_decoderblock_pb_kernel(tc, h2, w_ff1, b_ff1, w_ff2, b_ff2, out):
+    nc = tc.nc
+
+    h_view = h2.flatten_outer_dims().rearrange("(r i) d -> r (i d)", i=TOKEN_TILES)
+    out_view = out.flatten_outer_dims().rearrange("(r i) d -> r i d", i=TOKEN_TILES)
+    w1_view = w_ff1.rearrange("(q p e) d -> p q (e d)", p=P, e=PAIR)
+    b1_view = b_ff1.rearrange("(q x) -> q x", x=PAIR * P)
+    b2_view = b_ff2.rearrange("(o d) -> o d", o=1)
+
+    with ExitStack() as ctx:
+        keep = ctx.enter_context(tc.tile_pool(name="keep", bufs=1))
+        ring = ctx.enter_context(tc.tile_pool(name="ring", bufs=3))
+        psum = ctx.enter_context(tc.psum_pool(name="psum", bufs=8))
+
+        h_sb = keep.tile([P, TOKEN_TILES * D], BF16)
+        w1_sb = keep.tile([P, F_TILES * D], BF16)
+        w2_sb = keep.tile([P, D_TILES * F], BF16)
+
+        h_grouped = keep.tile([P, TOKENS * PACK], BF16, align_bytes=64)
+        w1_grouped = keep.tile([P, F * PACK], BF16, align_bytes=64)
+        w2_grouped = keep.tile([P, GROUPS * D * PACK], BF16, align_bytes=64)
+
+        h_codes = keep.tile([P, TOKENS], U32, align_bytes=64)
+        h_scales = keep.tile([P, TOKENS], U8, align_bytes=64)
+        w1_codes = keep.tile([P, F], U32, align_bytes=64)
+        w1_scales = keep.tile([P, F], U8, align_bytes=64)
+        w2_codes = keep.tile([P, GROUPS, D], U32, align_bytes=64)
+        w2_scales = keep.tile([P, GROUPS, D], U8, align_bytes=64)
+        a_codes = keep.tile([P, GROUPS, TOKENS], U32, align_bytes=64)
+        a_scales = keep.tile([P, GROUPS, TOKENS], U8, align_bytes=64)
+
+        resid = keep.tile([P, TOKEN_TILES, D], F32)
+        t_sb = keep.tile([P, TOKEN_TILES, D], F32)
+        squares = keep.tile([P, TOKEN_TILES, D], BF16)
+        sum_cols = keep.tile([P, TOKEN_TILES], F32)
+        sq_cols = keep.tile([P, TOKEN_TILES], F32)
+
+        ident = keep.tile([P, P], F32)
+        ones_bf = keep.tile([P, P], BF16)
+        mean_w = keep.tile([P, P], F32)
+        eps_col = keep.tile([P, 1], F32)
+        warm = keep.tile([P, 1], F32)
+        b1_rows = keep.tile([P, PAIR * P], BF16)
+        b1_words = keep.tile([P, F_TILES // PAIR], F32)
+        b1_col = keep.tile([P, F_TILES], F32)
+        b2_row = keep.tile([P, D], BF16)
+        b2_all = keep.tile([P, D], F32)
+
+        nc.vector.memset(b1_rows[:], 0.0)
+        nc.vector.memset(b2_row[:], 0.0)
+        nc.vector.memset(eps_col[:], EPS)
+        nc.vector.memset(ones_bf[:], 1.0)
+        nc.vector.memset(mean_w[:], 1.0 / (TOKENS * D))
+        make_identity(nc, ident[:])
+
+        nc.scalar.dma_start(out=b1_rows[0 : F_TILES // PAIR, :], in_=b1_view)
+        nc.scalar.dma_start(out=b2_row[0:1, :], in_=b2_view)
+        nc.scalar.activation(out=warm[:], in_=eps_col[:], func=ACT.Sqrt)
+
+        def load_h(half):
+            for pair in range(HALF_TILES // 2):
+                first = (half * HALF_TILES + 2 * pair) * D
+                nc.sync.dma_start(out=h_sb[:, first : first + 2 * D], in_=h_view[:, first : first + 2 * D])
+
+        def load_w1(g):
+            nc.sync.dma_start(
+                out=w1_sb[:, g * PACK * D : (g + 1) * PACK * D].rearrange("p (q x) -> p q x", q=PAIR),
+                in_=w1_view[:, PAIR * g : PAIR * (g + 1), :],
+            )
+
+        def load_w2(c):
+            nc.sync.dma_start(out=w2_sb[:, c * F : (c + 1) * F], in_=w_ff2[c * P : (c + 1) * P, :])
+
+        load_h(0)
+        for g in range(GROUPS):
+            load_w1(g)
+        load_h(1)
+        for c in range(D_TILES):
+            load_w2(c)
+
+        def new_bank():
+            return psum.tile([P, BANK], F32, name="bank", tag="bank")
+
+        def transpose_words(bank, slot, src):
+            nc.tensor.transpose(bank[:, slot * P : (slot + 1) * P], src.bitcast(F32), ident[:])
+
+        def interleaved(bank):
+            return bank[:].rearrange("p (x k r) -> p x r k", x=2, k=PAIR)
+
+        def as_words(grouped_cols):
+            return grouped_cols.bitcast(F32).rearrange("p (x r k) -> p x r k", x=2, k=PAIR)
+
+        def quantise(grouped_cols, codes, scales):
+            nc.vector.quantize_mx(out=codes.bitcast(FP8X4), scales=scales, in_=grouped_cols)
+
+        def transpose_h(half):
+            for pair in range(HALF_TILES // 2):
+                i0 = half * HALF_TILES + 2 * pair
+                bank = new_bank()
+                for x in range(2):
+                    for k in range(PAIR):
+                        first = (i0 + x) * D + k * PAIR * P
+                        transpose_words(bank, 2 * x + k, h_sb[:, first : first + PAIR * P])
+                cols = slice(i0 * P * PACK, (i0 + 2) * P * PACK)
+                nc.scalar.copy(out=as_words(h_grouped[:, cols]), in_=interleaved(bank))
+
+        def quantise_h(half):
+            tok = slice(half * HALF_TOKENS, (half + 1) * HALF_TOKENS)
+            quantise(
+                h_grouped[:, half * HALF_TOKENS * PACK : (half + 1) * HALF_TOKENS * PACK],
+                h_codes[:, tok],
+                h_scales[:, tok],
+            )
+
+        def prepare_biases():
+            bank = new_bank()
+            transpose_words(bank, 0, b1_rows[:])
+            nc.vector.tensor_copy(out=b1_words[:], in_=bank[:, 0 : F_TILES // PAIR])
+            spread = new_bank()
+            nc.tensor.matmul(out=spread[:], lhsT=ones_bf[:], rhs=b2_row[:], start=True, stop=True)
+            nc.vector.tensor_copy(out=b2_all[:], in_=spread[:])
+            nc.vector.tensor_copy(out=b1_col[:], in_=b1_words[:].bitcast(BF16))
+
+        def transpose_w1(g):
+            for q in range(PAIR * g, PAIR * (g + 1)):
+                bank = new_bank()
+                for e in range(PAIR):
+                    for k in range(PAIR):
+                        first = (PAIR * q + e) * D + k * PAIR * P
+                        transpose_words(bank, 2 * e + k, w1_sb[:, first : first + PAIR * P])
+                cols = slice(q * 2 * P * PACK, (q + 1) * 2 * P * PACK)
+                nc.scalar.copy(out=as_words(w1_grouped[:, cols]), in_=interleaved(bank))
+
+        def quantise_w1(g):
+            quantise(
+                w1_grouped[:, g * K_PASS * PACK : (g + 1) * K_PASS * PACK],
+                w1_codes[:, g * K_PASS : (g + 1) * K_PASS],
+                w1_scales[:, g * K_PASS : (g + 1) * K_PASS],
+            )
+
+        w2_words = w2_grouped[:].bitcast(F32).rearrange("p (g d k) -> p g d k", g=GROUPS, k=PAIR)
+
+        def transpose_w2_rows(c):
+            for g0 in range(0, GROUPS, 2):
+                bank = new_bank()
+                for x in range(2):
+                    for k in range(PAIR):
+                        first = c * F + (g0 + x) * K_PASS + k * PAIR * P
+                        transpose_words(bank, 2 * x + k, w2_sb[:, first : first + PAIR * P])
+                nc.scalar.copy(
+                    out=w2_words[:, g0 : g0 + 2, c * P : (c + 1) * P, :], in_=interleaved(bank)
+                )
+
+        def quantise_w2(g):
+            quantise(
+                w2_grouped[:, g * D * PACK : (g + 1) * D * PACK], w2_codes[:, g, :], w2_scales[:, g, :]
+            )
+
+        def add_bias_to_residual(i):
+            nc.vector.tensor_tensor(
+                out=resid[:, i, :], in0=h_sb[:, i * D : (i + 1) * D], in1=b2_all[:], op=ALU.add
+            )
+
+        a_rows = {}
+        a_grouped = {}
+        open_sums = {}
+
+        def first_matmul(unit):
+            half, g = divmod(unit, GROUPS)
+            tok = slice(half * HALF_TOKENS, (half + 1) * HALF_TOKENS)
+            a_rows[unit] = ring.tile([P, PACK, HALF_TOKENS], BF16, name="a_rows")
+            for v in range(PACK):
+                j = PACK * g + v
+                bank = new_bank()
+                nc.tensor.matmul_mx(
+                    out=bank[:],
+                    lhsT=w1_codes[:, j * P : (j + 1) * P].bitcast(FP8X4),
+                    lhsT_scale=w1_scales[:, j * P : (j + 1) * P],
+                    rhs=h_codes[:, tok].bitcast(FP8X4),
+                    rhs_scale=h_scales[:, tok],
+                    start=True,
+                    stop=True,
+                )
+                if half == 0 and v == PACK - 1:
+                    nc.vector.tensor_scalar(
+                        out=a_rows[unit][:, v, :],
+                        in0=bank[:],
+                        scalar1=b1_col[:, j : j + 1],
+                        scalar2=0.0,
+                        op0=ALU.add,
+                        op1=ALU.max,
+                    )
+                else:
+                    nc.scalar.activation(
+                        out=a_rows[unit][:, v, :],
+                        in_=bank[:],
+                        func=ACT.Relu,
+                        bias=b1_col[:, j : j + 1],
+                        scale=1.0,
+                    )
+
+        def regroup(unit):
+            a_grouped[unit] = ring.tile([P, HALF_TOKENS, PACK], BF16, name="a_grouped", align_bytes=64)
+            nc.vector.tensor_copy(
+                out=a_grouped[unit][:].rearrange("p (c n) v -> p c v n", n=4),
+                in_=a_rows[unit][:].rearrange("p v (c n) -> p c v n", n=4),
+            )
+
+        def quantise_a(unit):
+            half, g = divmod(unit, GROUPS)
+            tok = slice(half * HALF_TOKENS, (half + 1) * HALF_TOKENS)
+            quantise(
+                a_grouped[unit][:].rearrange("p n v -> p (n v)"), a_codes[:, g, tok], a_scales[:, g, tok]
+            )
+
+        def second_matmul(unit):
+            half, g = divmod(unit, GROUPS)
+            if g == 0:
+                open_sums[half] = [new_bank() for x in range(HALF_TILES)]
+            for x in range(HALF_TILES):
+                i = half * HALF_TILES + x
+                nc.tensor.matmul_mx(
+                    out=open_sums[half][x][:],
+                    lhsT=a_codes[:, g, i * P : (i + 1) * P].bitcast(FP8X4),
+                    lhsT_scale=a_scales[:, g, i * P : (i + 1) * P],
+                    rhs=w2_codes[:, g, :].bitcast(FP8X4),
+                    rhs_scale=w2_scales[:, g, :],
+                    start=(g == 0),
+                    stop=(g == GROUPS - 1),
+                )
+
+        def add_residual(i):
+            nc.vector.scalar_tensor_tensor(
+                out=t_sb[:, i, :],
+                in0=open_sums[i // HALF_TILES][i % HALF_TILES][:],
+                scalar=1.0,
+                in1=resid[:, i, :],
+                op0=ALU.mult,
+                op1=ALU.add,
+                accum_out=sum_cols[:, i : i + 1],
+            )
+
+        def sum_squares(i):
+            nc.scalar.activation(
+                out=squares[:, i, :], in_=t_sb[:, i, :], func=ACT.Square, accum_out=sq_cols[:, i : i + 1]
+            )
+
+        ctx.enter_context(tc.manual_schedule())
+        first_half = range(HALF_TILES)
+        second_half = range(HALF_TILES, TOKEN_TILES)
+
+        prepare_biases()
+        transpose_h(0)
+        add_bias_to_residual(0)
+        add_bias_to_residual(1)
+        quantise_h(0)
+        transpose_w1(0)
+        add_bias_to_residual(2)
+        quantise_w1(0)
+        transpose_w1(1)
+        add_bias_to_residual(3)
+        quantise_w1(1)
+
+        first_matmul(0)
+        transpose_w1(2)
+        transpose_w1(3)
+        regroup(0)
+        quantise_w1(2)
+        quantise_a(0)
+        quantise_w1(3)
+
+        first_matmul(1)
+        transpose_h(1)
+        for c in range(D_TILES):
+            transpose_w2_rows(c)
+        regroup(1)
+        quantise_h(1)
+        quantise_a(1)
+        for i in second_half:
+            add_bias_to_residual(i)
+        for g in range(GROUPS):
+            quantise_w2(g)
+
+        for unit in range(LAG, UNITS):
+            first_matmul(unit)
+            second_matmul(unit - LAG)
+            regroup(unit)
+            if unit - LAG == GROUPS - 1:
+                for i in first_half:
+                    add_residual(i)
+            quantise_a(unit)
+        for i in first_half:
+            sum_squares(i)
+        for unit in range(UNITS - LAG, UNITS):
+            second_matmul(unit)
+        for i in second_half:
+            add_residual(i)
+            sum_squares(i)
+
+        moments_ps = new_bank()
+        nc.tensor.matmul(
+            out=moments_ps[:, 0:TOKEN_TILES], lhsT=mean_w[:], rhs=sum_cols[:], start=True, stop=True
+        )
+        nc.tensor.matmul(
+            out=moments_ps[:, TOKEN_TILES : 2 * TOKEN_TILES],
+            lhsT=mean_w[:],
+            rhs=sq_cols[:],
+            start=True,
+            stop=True,
+        )
+        moments = keep.tile([P, 2], F32)
+        nc.vector.tensor_reduce(
+            out=moments[:],
+            in_=moments_ps[:, 0 : 2 * TOKEN_TILES].rearrange("p (s i) -> p s i", i=TOKEN_TILES),
+            axis=AXIS.X,
+            op=ALU.add,
+        )
+        mean = moments[:, 0:1]
+        neg_var = keep.tile([P, 1], F32)
+        nc.vector.scalar_tensor_tensor(
+            out=neg_var[:], in0=mean, scalar=mean, in1=moments[:, 1:2], op0=ALU.mult, op1=ALU.subtract
+        )
+        std = keep.tile([P, 1], F32)
+        nc.scalar.activation(out=std[:], in_=neg_var[:], func=ACT.Sqrt, scale=-1.0, bias=eps_col[:])
+        rstd = keep.tile([P, 1], F32)
+        nc.vector.reciprocal(out=rstd[:], in_=std[:])
+        for i in range(TOKEN_TILES):
+            nc.vector.tensor_scalar(
+                out=t_sb[:, i, :],
+                in0=t_sb[:, i, :],
+                scalar1=mean,
+                scalar2=rstd[:],
+                op0=ALU.subtract,
+                op1=ALU.mult,
+            )
+            queue = nc.sync if i % 2 == 0 else nc.scalar
+            queue.dma_start(out=out_view[:, i, :], in_=t_sb[:, i, :])

@@ -29,6 +29,8 @@ HALF_TILES = HALF_TOKENS // P
 GROUPS = F // K_PASS
 F_TILES = F // P
 D_TILES = D // P
+B1_ROWS = F // (PAIR * P)
+B2_ROWS = D // (PAIR * P)
 UNITS = 2 * GROUPS
 LAG = 2
 
@@ -41,8 +43,9 @@ def tile_decoderblock_pb_kernel(tc, h2, w_ff1, b_ff1, w_ff2, b_ff2, out):
     h_view = h2.flatten_outer_dims().rearrange("(r i) d -> r (i d)", i=TOKEN_TILES)
     out_view = out.flatten_outer_dims().rearrange("(r i) d -> r i d", i=TOKEN_TILES)
     w1_view = w_ff1.rearrange("(q p e) d -> p q (e d)", p=P, e=PAIR)
+    w2_view = w_ff2.rearrange("(k p e) f -> p k (e f)", p=P, e=PAIR)
     b1_view = b_ff1.rearrange("(q x) -> q x", x=PAIR * P)
-    b2_view = b_ff2.rearrange("(o d) -> o d", o=1)
+    b2_view = b_ff2.rearrange("(k x) -> k x", x=PAIR * P)
 
     with ExitStack() as ctx:
         keep = ctx.enter_context(tc.tile_pool(name="keep", bufs=1))
@@ -66,32 +69,26 @@ def tile_decoderblock_pb_kernel(tc, h2, w_ff1, b_ff1, w_ff2, b_ff2, out):
         a_codes = keep.tile([P, GROUPS, TOKENS], U32, align_bytes=64)
         a_scales = keep.tile([P, GROUPS, TOKENS], U8, align_bytes=64)
 
-        resid = keep.tile([P, TOKEN_TILES, D], F32)
-        t_sb = keep.tile([P, TOKEN_TILES, D], F32)
-        squares = keep.tile([P, TOKEN_TILES, D], BF16)
-        sum_cols = keep.tile([P, TOKEN_TILES], F32)
-        sq_cols = keep.tile([P, TOKEN_TILES], F32)
+        t_rows = keep.tile([P, D_TILES, TOKENS], F32)
+        squares = keep.tile([P, D_TILES, TOKENS], BF16)
+        y_sb = keep.tile([P, TOKEN_TILES, D], F32)
+        partial = keep.tile([P, 2, 2 * D_TILES], F32)
 
         ident = keep.tile([P, P], F32)
-        ones_bf = keep.tile([P, P], BF16)
         mean_w = keep.tile([P, P], F32)
         eps_col = keep.tile([P, 1], F32)
         warm = keep.tile([P, 1], F32)
-        b1_rows = keep.tile([P, PAIR * P], BF16)
-        b1_words = keep.tile([P, F_TILES // PAIR], F32)
-        b1_col = keep.tile([P, F_TILES], F32)
-        b2_row = keep.tile([P, D], BF16)
-        b2_all = keep.tile([P, D], F32)
+        bias_rows = keep.tile([P, PAIR * P], BF16)
+        bias_words = keep.tile([P, B1_ROWS + B2_ROWS], F32)
+        bias_col = keep.tile([P, F_TILES + D_TILES], F32)
 
-        nc.vector.memset(b1_rows[:], 0.0)
-        nc.vector.memset(b2_row[:], 0.0)
+        nc.vector.memset(bias_rows[:], 0.0)
         nc.vector.memset(eps_col[:], EPS)
-        nc.vector.memset(ones_bf[:], 1.0)
         nc.vector.memset(mean_w[:], 1.0 / (TOKENS * D))
         make_identity(nc, ident[:])
 
-        nc.scalar.dma_start(out=b1_rows[0 : F_TILES // PAIR, :], in_=b1_view)
-        nc.scalar.dma_start(out=b2_row[0:1, :], in_=b2_view)
+        nc.scalar.dma_start(out=bias_rows[0:B1_ROWS, :], in_=b1_view)
+        nc.scalar.dma_start(out=bias_rows[B1_ROWS : B1_ROWS + B2_ROWS, :], in_=b2_view)
         nc.scalar.activation(out=warm[:], in_=eps_col[:], func=ACT.Sqrt)
 
         def load_h(half):
@@ -106,7 +103,8 @@ def tile_decoderblock_pb_kernel(tc, h2, w_ff1, b_ff1, w_ff2, b_ff2, out):
             )
 
         def load_w2(c):
-            nc.sync.dma_start(out=w2_sb[:, c * F : (c + 1) * F], in_=w_ff2[c * P : (c + 1) * P, :])
+            k, e = divmod(c, PAIR)
+            nc.sync.dma_start(out=w2_sb[:, c * F : (c + 1) * F], in_=w2_view[:, k, e * F : (e + 1) * F])
 
         load_h(0)
         for g in range(GROUPS):
@@ -139,7 +137,7 @@ def tile_decoderblock_pb_kernel(tc, h2, w_ff1, b_ff1, w_ff2, b_ff2, out):
                         first = (i0 + x) * D + k * PAIR * P
                         transpose_words(bank, 2 * x + k, h_sb[:, first : first + PAIR * P])
                 cols = slice(i0 * P * PACK, (i0 + 2) * P * PACK)
-                nc.scalar.copy(out=as_words(h_grouped[:, cols]), in_=interleaved(bank))
+                nc.vector.tensor_copy(out=as_words(h_grouped[:, cols]), in_=interleaved(bank))
 
         def quantise_h(half):
             tok = slice(half * HALF_TOKENS, (half + 1) * HALF_TOKENS)
@@ -151,12 +149,9 @@ def tile_decoderblock_pb_kernel(tc, h2, w_ff1, b_ff1, w_ff2, b_ff2, out):
 
         def prepare_biases():
             bank = new_bank()
-            transpose_words(bank, 0, b1_rows[:])
-            nc.vector.tensor_copy(out=b1_words[:], in_=bank[:, 0 : F_TILES // PAIR])
-            spread = new_bank()
-            nc.tensor.matmul(out=spread[:], lhsT=ones_bf[:], rhs=b2_row[:], start=True, stop=True)
-            nc.vector.tensor_copy(out=b2_all[:], in_=spread[:])
-            nc.vector.tensor_copy(out=b1_col[:], in_=b1_words[:].bitcast(BF16))
+            transpose_words(bank, 0, bias_rows[:])
+            nc.vector.tensor_copy(out=bias_words[:], in_=bank[:, 0 : B1_ROWS + B2_ROWS])
+            nc.vector.tensor_copy(out=bias_col[:], in_=bias_words[:].bitcast(BF16))
 
         def transpose_w1(g):
             for q in range(PAIR * g, PAIR * (g + 1)):
@@ -193,11 +188,6 @@ def tile_decoderblock_pb_kernel(tc, h2, w_ff1, b_ff1, w_ff2, b_ff2, out):
                 w2_grouped[:, g * D * PACK : (g + 1) * D * PACK], w2_codes[:, g, :], w2_scales[:, g, :]
             )
 
-        def add_bias_to_residual(i):
-            nc.vector.tensor_tensor(
-                out=resid[:, i, :], in0=h_sb[:, i * D : (i + 1) * D], in1=b2_all[:], op=ALU.add
-            )
-
         a_rows = {}
         a_grouped = {}
         open_sums = {}
@@ -218,11 +208,11 @@ def tile_decoderblock_pb_kernel(tc, h2, w_ff1, b_ff1, w_ff2, b_ff2, out):
                     start=True,
                     stop=True,
                 )
-                if half == 0 and v == PACK - 1:
+                if half == 0 and v == 0:
                     nc.vector.tensor_scalar(
                         out=a_rows[unit][:, v, :],
                         in0=bank[:],
-                        scalar1=b1_col[:, j : j + 1],
+                        scalar1=bias_col[:, j : j + 1],
                         scalar2=0.0,
                         op0=ALU.add,
                         op1=ALU.max,
@@ -232,70 +222,86 @@ def tile_decoderblock_pb_kernel(tc, h2, w_ff1, b_ff1, w_ff2, b_ff2, out):
                         out=a_rows[unit][:, v, :],
                         in_=bank[:],
                         func=ACT.Relu,
-                        bias=b1_col[:, j : j + 1],
+                        bias=bias_col[:, j : j + 1],
                         scale=1.0,
                     )
 
+        part_tokens = HALF_TOKENS // 2
+
         def regroup(unit):
             a_grouped[unit] = ring.tile([P, HALF_TOKENS, PACK], BF16, name="a_grouped", align_bytes=64)
-            nc.vector.tensor_copy(
-                out=a_grouped[unit][:].rearrange("p (c n) v -> p c v n", n=4),
-                in_=a_rows[unit][:].rearrange("p v (c n) -> p c v n", n=4),
-            )
+            for part in range(2):
+                tok = slice(part * part_tokens, (part + 1) * part_tokens)
+                nc.vector.tensor_copy(
+                    out=a_grouped[unit][:, tok, :].rearrange("p (c n) v -> p c v n", n=4),
+                    in_=a_rows[unit][:, :, tok].rearrange("p v (c n) -> p c v n", n=4),
+                )
 
         def quantise_a(unit):
             half, g = divmod(unit, GROUPS)
-            tok = slice(half * HALF_TOKENS, (half + 1) * HALF_TOKENS)
-            quantise(
-                a_grouped[unit][:].rearrange("p n v -> p (n v)"), a_codes[:, g, tok], a_scales[:, g, tok]
-            )
+            for part in range(2):
+                tok = slice(part * part_tokens, (part + 1) * part_tokens)
+                first = half * HALF_TOKENS + part * part_tokens
+                quantise(
+                    a_grouped[unit][:, tok, :].rearrange("p n v -> p (n v)"),
+                    a_codes[:, g, first : first + part_tokens],
+                    a_scales[:, g, first : first + part_tokens],
+                )
 
         def second_matmul(unit):
             half, g = divmod(unit, GROUPS)
+            tok = slice(half * HALF_TOKENS, (half + 1) * HALF_TOKENS)
             if g == 0:
-                open_sums[half] = [new_bank() for x in range(HALF_TILES)]
-            for x in range(HALF_TILES):
-                i = half * HALF_TILES + x
+                open_sums[half] = [new_bank() for c in range(D_TILES)]
+            for c in range(D_TILES):
                 nc.tensor.matmul_mx(
-                    out=open_sums[half][x][:],
-                    lhsT=a_codes[:, g, i * P : (i + 1) * P].bitcast(FP8X4),
-                    lhsT_scale=a_scales[:, g, i * P : (i + 1) * P],
-                    rhs=w2_codes[:, g, :].bitcast(FP8X4),
-                    rhs_scale=w2_scales[:, g, :],
+                    out=open_sums[half][c][:],
+                    lhsT=w2_codes[:, g, c * P : (c + 1) * P].bitcast(FP8X4),
+                    lhsT_scale=w2_scales[:, g, c * P : (c + 1) * P],
+                    rhs=a_codes[:, g, tok].bitcast(FP8X4),
+                    rhs_scale=a_scales[:, g, tok],
                     start=(g == 0),
                     stop=(g == GROUPS - 1),
                 )
 
-        def add_residual(i):
+        h_by_value = h_grouped[:].rearrange("p (n v) -> p n v", v=PACK)
+
+        def add_residual(half, c):
+            tok = slice(half * HALF_TOKENS, (half + 1) * HALF_TOKENS)
             nc.vector.scalar_tensor_tensor(
-                out=t_sb[:, i, :],
-                in0=open_sums[i // HALF_TILES][i % HALF_TILES][:],
-                scalar=1.0,
-                in1=resid[:, i, :],
-                op0=ALU.mult,
+                out=t_rows[:, c, tok],
+                in0=open_sums[half][c][:],
+                scalar=bias_col[:, F_TILES + c : F_TILES + c + 1],
+                in1=h_by_value[:, tok, c],
+                op0=ALU.add,
                 op1=ALU.add,
-                accum_out=sum_cols[:, i : i + 1],
+                accum_out=partial[:, 0, half * D_TILES + c : half * D_TILES + c + 1],
             )
 
-        def sum_squares(i):
+        def sum_squares(half, c):
+            tok = slice(half * HALF_TOKENS, (half + 1) * HALF_TOKENS)
             nc.scalar.activation(
-                out=squares[:, i, :], in_=t_sb[:, i, :], func=ACT.Square, accum_out=sq_cols[:, i : i + 1]
+                out=squares[:, c, tok],
+                in_=t_rows[:, c, tok],
+                func=ACT.Square,
+                accum_out=partial[:, 1, half * D_TILES + c : half * D_TILES + c + 1],
             )
 
-        ctx.enter_context(tc.manual_schedule())
-        first_half = range(HALF_TILES)
-        second_half = range(HALF_TILES, TOKEN_TILES)
+        t_banks = {}
 
-        prepare_biases()
+        def transpose_back(i):
+            t_banks[i] = new_bank()
+            for c in range(D_TILES):
+                nc.tensor.transpose(
+                    t_banks[i][:, c * P : (c + 1) * P], t_rows[:, c, i * P : (i + 1) * P], ident[:]
+                )
+
         transpose_h(0)
-        add_bias_to_residual(0)
-        add_bias_to_residual(1)
         quantise_h(0)
         transpose_w1(0)
-        add_bias_to_residual(2)
         quantise_w1(0)
         transpose_w1(1)
-        add_bias_to_residual(3)
+        prepare_biases()
         quantise_w1(1)
 
         first_matmul(0)
@@ -313,8 +319,6 @@ def tile_decoderblock_pb_kernel(tc, h2, w_ff1, b_ff1, w_ff2, b_ff2, out):
         regroup(1)
         quantise_h(1)
         quantise_a(1)
-        for i in second_half:
-            add_bias_to_residual(i)
         for g in range(GROUPS):
             quantise_w2(g)
 
@@ -323,32 +327,33 @@ def tile_decoderblock_pb_kernel(tc, h2, w_ff1, b_ff1, w_ff2, b_ff2, out):
             second_matmul(unit - LAG)
             regroup(unit)
             if unit - LAG == GROUPS - 1:
-                for i in first_half:
-                    add_residual(i)
+                for c in range(D_TILES):
+                    add_residual(0, c)
             quantise_a(unit)
-        for i in first_half:
-            sum_squares(i)
+        for c in range(D_TILES):
+            sum_squares(0, c)
         for unit in range(UNITS - LAG, UNITS):
             second_matmul(unit)
-        for i in second_half:
-            add_residual(i)
-            sum_squares(i)
+        for i in range(HALF_TILES):
+            transpose_back(i)
+        for c in range(D_TILES):
+            add_residual(1, c)
+            sum_squares(1, c)
 
         moments_ps = new_bank()
         nc.tensor.matmul(
-            out=moments_ps[:, 0:TOKEN_TILES], lhsT=mean_w[:], rhs=sum_cols[:], start=True, stop=True
-        )
-        nc.tensor.matmul(
-            out=moments_ps[:, TOKEN_TILES : 2 * TOKEN_TILES],
+            out=moments_ps[:, 0 : 4 * D_TILES],
             lhsT=mean_w[:],
-            rhs=sq_cols[:],
+            rhs=partial[:].rearrange("p s x -> p (s x)"),
             start=True,
             stop=True,
         )
+        for i in range(HALF_TILES, TOKEN_TILES):
+            transpose_back(i)
         moments = keep.tile([P, 2], F32)
         nc.vector.tensor_reduce(
             out=moments[:],
-            in_=moments_ps[:, 0 : 2 * TOKEN_TILES].rearrange("p (s i) -> p s i", i=TOKEN_TILES),
+            in_=moments_ps[:, 0 : 4 * D_TILES].rearrange("p (s x) -> p s x", s=2),
             axis=AXIS.X,
             op=ALU.add,
         )
@@ -361,14 +366,20 @@ def tile_decoderblock_pb_kernel(tc, h2, w_ff1, b_ff1, w_ff2, b_ff2, out):
         nc.scalar.activation(out=std[:], in_=neg_var[:], func=ACT.Sqrt, scale=-1.0, bias=eps_col[:])
         rstd = keep.tile([P, 1], F32)
         nc.vector.reciprocal(out=rstd[:], in_=std[:])
+        shift = keep.tile([P, 1], F32)
+        nc.vector.scalar_tensor_tensor(
+            out=shift[:], in0=mean, scalar=-1.0, in1=rstd[:], op0=ALU.mult, op1=ALU.mult
+        )
         for i in range(TOKEN_TILES):
-            nc.vector.tensor_scalar(
-                out=t_sb[:, i, :],
-                in0=t_sb[:, i, :],
-                scalar1=mean,
-                scalar2=rstd[:],
-                op0=ALU.subtract,
-                op1=ALU.mult,
-            )
-            queue = nc.sync if i % 2 == 0 else nc.scalar
-            queue.dma_start(out=out_view[:, i, :], in_=t_sb[:, i, :])
+            from_bank = t_banks[i][:].rearrange("r (k e p) -> r k p e", k=2, e=PAIR)
+            to_sbuf = y_sb[:, i, :].rearrange("r (k p e) -> r k p e", k=2, e=PAIR)
+            if i % 2 == 0:
+                nc.vector.tensor_scalar(
+                    out=to_sbuf, in0=from_bank, scalar1=mean, scalar2=rstd[:], op0=ALU.subtract, op1=ALU.mult
+                )
+                nc.sync.dma_start(out=out_view[:, i, :], in_=y_sb[:, i, :])
+            else:
+                nc.scalar.activation(
+                    out=to_sbuf, in_=from_bank, func=ACT.Identity, scale=rstd[:], bias=shift[:]
+                )
+                nc.scalar.dma_start(out=out_view[:, i, :], in_=y_sb[:, i, :])

@@ -96,19 +96,16 @@ def tile_decoderblock_pb_kernel(tc, h2, w_ff1, b_ff1, w_ff2, b_ff2, out):
                 first = (half * HALF_TILES + 2 * pair) * D
                 nc.sync.dma_start(out=h_sb[:, first : first + 2 * D], in_=h_view[:, first : first + 2 * D])
 
-        def load_w1(g):
-            nc.sync.dma_start(
-                out=w1_sb[:, g * PACK * D : (g + 1) * PACK * D].rearrange("p (q x) -> p q x", q=PAIR),
-                in_=w1_view[:, PAIR * g : PAIR * (g + 1), :],
-            )
+        def load_w1(q):
+            nc.sync.dma_start(out=w1_sb[:, q * PAIR * D : (q + 1) * PAIR * D], in_=w1_view[:, q, :])
 
         def load_w2(c):
             k, e = divmod(c, PAIR)
             nc.sync.dma_start(out=w2_sb[:, c * F : (c + 1) * F], in_=w2_view[:, k, e * F : (e + 1) * F])
 
         load_h(0)
-        for g in range(GROUPS):
-            load_w1(g)
+        for q in range(F_TILES // PAIR):
+            load_w1(q)
         load_h(1)
         for c in range(D_TILES):
             load_w2(c)
@@ -128,6 +125,8 @@ def tile_decoderblock_pb_kernel(tc, h2, w_ff1, b_ff1, w_ff2, b_ff2, out):
         def quantise(grouped_cols, codes, scales):
             nc.vector.quantize_mx(out=codes.bitcast(FP8X4), scales=scales, in_=grouped_cols)
 
+        bank_cols = 2 * P
+
         def transpose_h(half):
             for pair in range(HALF_TILES // 2):
                 i0 = half * HALF_TILES + 2 * pair
@@ -140,12 +139,13 @@ def tile_decoderblock_pb_kernel(tc, h2, w_ff1, b_ff1, w_ff2, b_ff2, out):
                 nc.vector.tensor_copy(out=as_words(h_grouped[:, cols]), in_=interleaved(bank))
 
         def quantise_h(half):
-            tok = slice(half * HALF_TOKENS, (half + 1) * HALF_TOKENS)
-            quantise(
-                h_grouped[:, half * HALF_TOKENS * PACK : (half + 1) * HALF_TOKENS * PACK],
-                h_codes[:, tok],
-                h_scales[:, tok],
-            )
+            for pair in range(HALF_TILES // 2):
+                first = half * HALF_TOKENS + pair * bank_cols
+                quantise(
+                    h_grouped[:, first * PACK : (first + bank_cols) * PACK],
+                    h_codes[:, first : first + bank_cols],
+                    h_scales[:, first : first + bank_cols],
+                )
 
         def prepare_biases():
             bank = new_bank()
@@ -164,11 +164,13 @@ def tile_decoderblock_pb_kernel(tc, h2, w_ff1, b_ff1, w_ff2, b_ff2, out):
                 nc.scalar.copy(out=as_words(w1_grouped[:, cols]), in_=interleaved(bank))
 
         def quantise_w1(g):
-            quantise(
-                w1_grouped[:, g * K_PASS * PACK : (g + 1) * K_PASS * PACK],
-                w1_codes[:, g * K_PASS : (g + 1) * K_PASS],
-                w1_scales[:, g * K_PASS : (g + 1) * K_PASS],
-            )
+            for q in range(PAIR * g, PAIR * (g + 1)):
+                first = q * bank_cols
+                quantise(
+                    w1_grouped[:, first * PACK : (first + bank_cols) * PACK],
+                    w1_codes[:, first : first + bank_cols],
+                    w1_scales[:, first : first + bank_cols],
+                )
 
         w2_words = w2_grouped[:].bitcast(F32).rearrange("p (g d k) -> p g d k", g=GROUPS, k=PAIR)
 
@@ -296,6 +298,7 @@ def tile_decoderblock_pb_kernel(tc, h2, w_ff1, b_ff1, w_ff2, b_ff2, out):
                     t_banks[i][:, c * P : (c + 1) * P], t_rows[:, c, i * P : (i + 1) * P], ident[:]
                 )
 
+        ctx.enter_context(tc.manual_schedule())
         transpose_h(0)
         quantise_h(0)
         transpose_w1(0)

@@ -24,15 +24,16 @@ F = 2048
 EPS = 1e-5
 
 TOKEN_TILES = TOKENS // P
-HALF_TOKENS = TOKENS // 2
-HALF_TILES = HALF_TOKENS // P
 GROUPS = F // K_PASS
 F_TILES = F // P
 D_TILES = D // P
 B1_ROWS = F // (PAIR * P)
 B2_ROWS = D // (PAIR * P)
-UNITS = 2 * GROUPS
-LAG = 2
+
+HALF_TOKENS = TOKENS // 2
+BLOCK = P
+
+RV = ((0, 1),)
 
 FLOPS = 2 * TOKENS * D * F * 2
 
@@ -43,18 +44,18 @@ def tile_decoderblock_pb_kernel(tc, h2, w_ff1, b_ff1, w_ff2, b_ff2, out):
     h_view = h2.flatten_outer_dims().rearrange("(r i) d -> r (i d)", i=TOKEN_TILES)
     out_view = out.flatten_outer_dims().rearrange("(r i) d -> r i d", i=TOKEN_TILES)
     w1_view = w_ff1.rearrange("(q p e) d -> p q (e d)", p=P, e=PAIR)
-    w2_view = w_ff2.rearrange("(k p e) f -> p k (e f)", p=P, e=PAIR)
+    w2_view = w_ff2.rearrange("(k p e) f -> p k e f", p=P, e=PAIR)
     b1_view = b_ff1.rearrange("(q x) -> q x", x=PAIR * P)
     b2_view = b_ff2.rearrange("(k x) -> k x", x=PAIR * P)
 
     with ExitStack() as ctx:
         keep = ctx.enter_context(tc.tile_pool(name="keep", bufs=1))
         ring = ctx.enter_context(tc.tile_pool(name="ring", bufs=3))
-        psum = ctx.enter_context(tc.psum_pool(name="psum", bufs=8))
+        psum = ctx.enter_context(tc.psum_pool(name="psum", bufs=1))
 
         h_sb = keep.tile([P, TOKEN_TILES * D], BF16)
         w1_sb = keep.tile([P, F_TILES * D], BF16)
-        w2_sb = keep.tile([P, D_TILES * F], BF16)
+        w2_sb = keep.tile([P, GROUPS, PAIR, PAIR, K_PASS], BF16)
 
         h_grouped = keep.tile([P, TOKENS * PACK], BF16, align_bytes=64)
         w1_grouped = keep.tile([P, F * PACK], BF16, align_bytes=64)
@@ -72,7 +73,8 @@ def tile_decoderblock_pb_kernel(tc, h2, w_ff1, b_ff1, w_ff2, b_ff2, out):
         t_rows = keep.tile([P, D_TILES, TOKENS], F32)
         squares = keep.tile([P, D_TILES, TOKENS], BF16)
         y_sb = keep.tile([P, TOKEN_TILES, D], F32)
-        partial = keep.tile([P, 2, 2 * D_TILES], F32)
+        COLS = 16
+        partial = keep.tile([P, 2, COLS], F32)
 
         ident = keep.tile([P, P], F32)
         mean_w = keep.tile([P, P], F32)
@@ -85,33 +87,51 @@ def tile_decoderblock_pb_kernel(tc, h2, w_ff1, b_ff1, w_ff2, b_ff2, out):
         nc.vector.memset(bias_rows[:], 0.0)
         nc.vector.memset(eps_col[:], EPS)
         nc.vector.memset(mean_w[:], 1.0 / (TOKENS * D))
+        nc.vector.memset(partial[:], 0.0)
         make_identity(nc, ident[:])
 
         nc.scalar.dma_start(out=bias_rows[0:B1_ROWS, :], in_=b1_view)
         nc.scalar.dma_start(out=bias_rows[B1_ROWS : B1_ROWS + B2_ROWS, :], in_=b2_view)
-        nc.scalar.activation(out=warm[:], in_=eps_col[:], func=ACT.Sqrt)
+        nc.scalar.activation(out=warm[:], in_=eps_col[:], func=ACT.Abs_reciprocal_sqrt)
 
-        def load_h(half):
-            for pair in range(HALF_TILES // 2):
-                first = (half * HALF_TILES + 2 * pair) * D
-                nc.sync.dma_start(out=h_sb[:, first : first + 2 * D], in_=h_view[:, first : first + 2 * D])
+        def load_h(i0, n):
+            nc.sync.dma_start(out=h_sb[:, i0 * D : (i0 + n) * D], in_=h_view[:, i0 * D : (i0 + n) * D])
 
         def load_w1(q):
             nc.sync.dma_start(out=w1_sb[:, q * PAIR * D : (q + 1) * PAIR * D], in_=w1_view[:, q, :])
 
-        def load_w2(c):
-            k, e = divmod(c, PAIR)
-            nc.sync.dma_start(out=w2_sb[:, c * F : (c + 1) * F], in_=w2_view[:, k, e * F : (e + 1) * F])
+        def load_w2(g):
+            for k in range(PAIR):
+                nc.sync.dma_start(
+                    out=w2_sb[:, g, k, :, :], in_=w2_view[:, k, :, g * K_PASS : (g + 1) * K_PASS]
+                )
 
-        load_h(0)
-        for q in range(F_TILES // PAIR):
-            load_w1(q)
-        load_h(1)
-        for c in range(D_TILES):
-            load_w2(c)
+        load_h(0, 1)
+        load_h(1, 1)
+        load_h(2, 2)
+        load_w1(0)
+        load_w1(1)
+        load_w1(2)
+        load_w1(3)
+        load_w2(0)
+        load_w1(4)
+        load_w1(5)
+        load_w2(1)
+        load_w1(6)
+        load_w1(7)
+        load_w2(2)
+        load_h(4, 4)
+        load_w2(3)
+
+        state = {"n": 0}
+
+        def bank_of(tag):
+            return psum.tile([P, BANK], F32, name=tag, tag=tag)
 
         def new_bank():
-            return psum.tile([P, BANK], F32, name="bank", tag="bank")
+            n = state["n"]
+            state["n"] = n + 1
+            return bank_of("work%d" % (n % 4))
 
         def transpose_words(bank, slot, src):
             nc.tensor.transpose(bank[:, slot * P : (slot + 1) * P], src.bitcast(F32), ident[:])
@@ -127,63 +147,62 @@ def tile_decoderblock_pb_kernel(tc, h2, w_ff1, b_ff1, w_ff2, b_ff2, out):
 
         bank_cols = 2 * P
 
-        def transpose_h(half):
-            for pair in range(HALF_TILES // 2):
-                i0 = half * HALF_TILES + 2 * pair
+        def copy_out(engine, out_, in_):
+            if engine == "v":
+                nc.vector.tensor_copy(out=out_, in_=in_)
+            else:
+                nc.scalar.copy(out=out_, in_=in_)
+
+        def transpose_h(pair, engine, bank=None):
+            i0 = 2 * pair
+            if bank is None:
                 bank = new_bank()
-                for x in range(2):
-                    for k in range(PAIR):
-                        first = (i0 + x) * D + k * PAIR * P
-                        transpose_words(bank, 2 * x + k, h_sb[:, first : first + PAIR * P])
-                cols = slice(i0 * P * PACK, (i0 + 2) * P * PACK)
-                nc.vector.tensor_copy(out=as_words(h_grouped[:, cols]), in_=interleaved(bank))
+            for x in range(2):
+                for k in range(PAIR):
+                    first = (i0 + x) * D + k * PAIR * P
+                    transpose_words(bank, 2 * x + k, h_sb[:, first : first + PAIR * P])
+            cols = slice(i0 * P * PACK, (i0 + 2) * P * PACK)
+            copy_out(engine, as_words(h_grouped[:, cols]), interleaved(bank))
 
-        def quantise_h(half):
-            for pair in range(HALF_TILES // 2):
-                first = half * HALF_TOKENS + pair * bank_cols
-                quantise(
-                    h_grouped[:, first * PACK : (first + bank_cols) * PACK],
-                    h_codes[:, first : first + bank_cols],
-                    h_scales[:, first : first + bank_cols],
-                )
+        def quantise_h(pair):
+            first = pair * bank_cols
+            quantise(
+                h_grouped[:, first * PACK : (first + bank_cols) * PACK],
+                h_codes[:, first : first + bank_cols],
+                h_scales[:, first : first + bank_cols],
+            )
 
-        def prepare_biases():
-            bank = new_bank()
+        def prepare_biases(bank):
             transpose_words(bank, 0, bias_rows[:])
             nc.vector.tensor_copy(out=bias_words[:], in_=bank[:, 0 : B1_ROWS + B2_ROWS])
             nc.vector.tensor_copy(out=bias_col[:], in_=bias_words[:].bitcast(BF16))
 
-        def transpose_w1(g):
-            for q in range(PAIR * g, PAIR * (g + 1)):
+        def transpose_w1(q, engine, bank=None):
+            if bank is None:
                 bank = new_bank()
-                for e in range(PAIR):
-                    for k in range(PAIR):
-                        first = (PAIR * q + e) * D + k * PAIR * P
-                        transpose_words(bank, 2 * e + k, w1_sb[:, first : first + PAIR * P])
-                cols = slice(q * 2 * P * PACK, (q + 1) * 2 * P * PACK)
-                nc.scalar.copy(out=as_words(w1_grouped[:, cols]), in_=interleaved(bank))
+            for e in range(PAIR):
+                for k in range(PAIR):
+                    first = (PAIR * q + e) * D + k * PAIR * P
+                    transpose_words(bank, 2 * e + k, w1_sb[:, first : first + PAIR * P])
+            cols = slice(q * 2 * P * PACK, (q + 1) * 2 * P * PACK)
+            copy_out(engine, as_words(w1_grouped[:, cols]), interleaved(bank))
 
-        def quantise_w1(g):
-            for q in range(PAIR * g, PAIR * (g + 1)):
-                first = q * bank_cols
-                quantise(
-                    w1_grouped[:, first * PACK : (first + bank_cols) * PACK],
-                    w1_codes[:, first : first + bank_cols],
-                    w1_scales[:, first : first + bank_cols],
-                )
+        def quantise_w1(q):
+            first = q * bank_cols
+            quantise(
+                w1_grouped[:, first * PACK : (first + bank_cols) * PACK],
+                w1_codes[:, first : first + bank_cols],
+                w1_scales[:, first : first + bank_cols],
+            )
 
-        w2_words = w2_grouped[:].bitcast(F32).rearrange("p (g d k) -> p g d k", g=GROUPS, k=PAIR)
-
-        def transpose_w2_rows(c):
-            for g0 in range(0, GROUPS, 2):
+        def transpose_w2(g, k, engine, bank=None):
+            if bank is None:
                 bank = new_bank()
-                for x in range(2):
-                    for k in range(PAIR):
-                        first = c * F + (g0 + x) * K_PASS + k * PAIR * P
-                        transpose_words(bank, 2 * x + k, w2_sb[:, first : first + PAIR * P])
-                nc.scalar.copy(
-                    out=w2_words[:, g0 : g0 + 2, c * P : (c + 1) * P, :], in_=interleaved(bank)
-                )
+            for e in range(PAIR):
+                for half in range(PAIR):
+                    transpose_words(bank, 2 * e + half, w2_sb[:, g, k, e, half * PAIR * P : (half + 1) * PAIR * P])
+            first = (g * D + k * bank_cols) * PACK
+            copy_out(engine, as_words(w2_grouped[:, first : first + bank_cols * PACK]), interleaved(bank))
 
         def quantise_w2(g):
             quantise(
@@ -194,195 +213,253 @@ def tile_decoderblock_pb_kernel(tc, h2, w_ff1, b_ff1, w_ff2, b_ff2, out):
         a_grouped = {}
         open_sums = {}
 
-        def first_matmul(unit):
-            half, g = divmod(unit, GROUPS)
-            tok = slice(half * HALF_TOKENS, (half + 1) * HALF_TOKENS)
+        def start_unit(unit):
             a_rows[unit] = ring.tile([P, PACK, HALF_TOKENS], BF16, name="a_rows")
-            for v in range(PACK):
-                j = PACK * g + v
-                bank = new_bank()
-                nc.tensor.matmul_mx(
-                    out=bank[:],
-                    lhsT=w1_codes[:, j * P : (j + 1) * P].bitcast(FP8X4),
-                    lhsT_scale=w1_scales[:, j * P : (j + 1) * P],
-                    rhs=h_codes[:, tok].bitcast(FP8X4),
-                    rhs_scale=h_scales[:, tok],
-                    start=True,
-                    stop=True,
-                )
-                if half == 0 and v == 0:
-                    nc.vector.tensor_scalar(
-                        out=a_rows[unit][:, v, :],
-                        in0=bank[:],
-                        scalar1=bias_col[:, j : j + 1],
-                        scalar2=0.0,
-                        op0=ALU.add,
-                        op1=ALU.max,
-                    )
-                else:
-                    nc.scalar.activation(
-                        out=a_rows[unit][:, v, :],
-                        in_=bank[:],
-                        func=ACT.Relu,
-                        bias=bias_col[:, j : j + 1],
-                        scale=1.0,
-                    )
-
-        part_tokens = HALF_TOKENS // 2
-
-        def regroup(unit):
             a_grouped[unit] = ring.tile([P, HALF_TOKENS, PACK], BF16, name="a_grouped", align_bytes=64)
-            for part in range(2):
-                tok = slice(part * part_tokens, (part + 1) * part_tokens)
-                nc.vector.tensor_copy(
-                    out=a_grouped[unit][:, tok, :].rearrange("p (c n) v -> p c v n", n=4),
-                    in_=a_rows[unit][:, :, tok].rearrange("p v (c n) -> p c v n", n=4),
-                )
 
-        def quantise_a(unit):
+        def first_pass(unit, v, first, width, bank, col):
             half, g = divmod(unit, GROUPS)
-            for part in range(2):
-                tok = slice(part * part_tokens, (part + 1) * part_tokens)
-                first = half * HALF_TOKENS + part * part_tokens
-                quantise(
-                    a_grouped[unit][:, tok, :].rearrange("p n v -> p (n v)"),
-                    a_codes[:, g, first : first + part_tokens],
-                    a_scales[:, g, first : first + part_tokens],
+            j = PACK * g + v
+            t0 = half * HALF_TOKENS + first
+            nc.tensor.matmul_mx(
+                out=bank[:, col : col + width],
+                lhsT=w1_codes[:, j * P : (j + 1) * P].bitcast(FP8X4),
+                lhsT_scale=w1_scales[:, j * P : (j + 1) * P],
+                rhs=h_codes[:, t0 : t0 + width].bitcast(FP8X4),
+                rhs_scale=h_scales[:, t0 : t0 + width],
+                start=True,
+                stop=True,
+            )
+
+        def relu_rows(unit, v, first, width, bank, col):
+            half, g = divmod(unit, GROUPS)
+            j = PACK * g + v
+            if (unit, v) in RV:
+                nc.vector.tensor_scalar(
+                    out=a_rows[unit][:, v, first : first + width],
+                    in0=bank[:, col : col + width],
+                    scalar1=bias_col[:, j : j + 1],
+                    scalar2=0.0,
+                    op0=ALU.add,
+                    op1=ALU.max,
                 )
+                return
+            nc.scalar.activation(
+                out=a_rows[unit][:, v, first : first + width],
+                in_=bank[:, col : col + width],
+                func=ACT.Relu,
+                bias=bias_col[:, j : j + 1],
+                scale=1.0,
+            )
+
+        def s_route(unit, values, first=0, width=HALF_TOKENS):
+            per_bank = BANK // width
+            for v0 in range(values[0], values[-1] + 1, per_bank):
+                bank = new_bank()
+                for x in range(per_bank):
+                    first_pass(unit, v0 + x, first, width, bank, x * width)
+                for x in range(per_bank):
+                    relu_rows(unit, v0 + x, first, width, bank, x * width)
+
+        def v_pass(unit, block):
+            half, g = divmod(unit, GROUPS)
+            bank = new_bank()
+            for v in range(PACK):
+                first_pass(unit, v, block * BLOCK, BLOCK, bank, v * BLOCK)
+            bias = bias_col[:, PACK * g : PACK * (g + 1)].unsqueeze(1).to_broadcast([P, BLOCK, PACK])
+            nc.vector.tensor_tensor(
+                out=a_grouped[unit][:, block * BLOCK : (block + 1) * BLOCK, :],
+                in0=bank[:].rearrange("p (v n) -> p n v", v=PACK),
+                in1=bias,
+                op=ALU.add,
+            )
+
+        def v_relu(unit, b0, b1):
+            part = a_grouped[unit][:, b0 * BLOCK : b1 * BLOCK, :].rearrange("p n v -> p (n v)")
+            nc.vector.tensor_scalar_max(out=part, in0=part, scalar1=0.0)
+
+        def regroup(unit, first, width):
+            tok = slice(first, first + width)
+            nc.vector.tensor_copy(
+                out=a_grouped[unit][:, tok, :].rearrange("p (c n) v -> p c v n", n=4),
+                in_=a_rows[unit][:, :, tok].rearrange("p v (c n) -> p c v n", n=4),
+            )
+
+        def quantise_a(unit, first, width):
+            half, g = divmod(unit, GROUPS)
+            col = half * HALF_TOKENS + first
+            quantise(
+                a_grouped[unit][:, first : first + width, :].rearrange("p n v -> p (n v)"),
+                a_codes[:, g, col : col + width],
+                a_scales[:, g, col : col + width],
+            )
+
+        def second_pass(key, g, c, first, width, bank=None):
+            if g == 0:
+                open_sums[key, c] = bank_of("sum%d" % c) if bank is None else bank
+            nc.tensor.matmul_mx(
+                out=open_sums[key, c][:, 0:width],
+                lhsT=w2_codes[:, g, c * P : (c + 1) * P].bitcast(FP8X4),
+                lhsT_scale=w2_scales[:, g, c * P : (c + 1) * P],
+                rhs=a_codes[:, g, first : first + width].bitcast(FP8X4),
+                rhs_scale=a_scales[:, g, first : first + width],
+                start=(g == 0),
+                stop=(g == GROUPS - 1),
+            )
 
         def second_matmul(unit):
             half, g = divmod(unit, GROUPS)
-            tok = slice(half * HALF_TOKENS, (half + 1) * HALF_TOKENS)
-            if g == 0:
-                open_sums[half] = [new_bank() for c in range(D_TILES)]
             for c in range(D_TILES):
-                nc.tensor.matmul_mx(
-                    out=open_sums[half][c][:],
-                    lhsT=w2_codes[:, g, c * P : (c + 1) * P].bitcast(FP8X4),
-                    lhsT_scale=w2_scales[:, g, c * P : (c + 1) * P],
-                    rhs=a_codes[:, g, tok].bitcast(FP8X4),
-                    rhs_scale=a_scales[:, g, tok],
-                    start=(g == 0),
-                    stop=(g == GROUPS - 1),
-                )
+                second_pass(half, g, c, half * HALF_TOKENS, HALF_TOKENS)
 
         h_by_value = h_grouped[:].rearrange("p (n v) -> p n v", v=PACK)
 
-        def add_residual(half, c):
-            tok = slice(half * HALF_TOKENS, (half + 1) * HALF_TOKENS)
+        def add_residual(key, c, first, width, col):
+            tok = slice(first, first + width)
             nc.vector.scalar_tensor_tensor(
                 out=t_rows[:, c, tok],
-                in0=open_sums[half][c][:],
+                in0=open_sums[key, c][:, 0:width],
                 scalar=bias_col[:, F_TILES + c : F_TILES + c + 1],
                 in1=h_by_value[:, tok, c],
                 op0=ALU.add,
                 op1=ALU.add,
-                accum_out=partial[:, 0, half * D_TILES + c : half * D_TILES + c + 1],
+                accum_out=partial[:, 0, col : col + 1],
             )
 
-        def sum_squares(half, c):
-            tok = slice(half * HALF_TOKENS, (half + 1) * HALF_TOKENS)
+        def sum_squares(c, first, width, col):
+            tok = slice(first, first + width)
             nc.scalar.activation(
                 out=squares[:, c, tok],
                 in_=t_rows[:, c, tok],
                 func=ACT.Square,
-                accum_out=partial[:, 1, half * D_TILES + c : half * D_TILES + c + 1],
+                accum_out=partial[:, 1, col : col + 1],
             )
 
         t_banks = {}
 
-        def transpose_back(i):
-            t_banks[i] = new_bank()
+        def transpose_back(i, tag):
+            t_banks[i] = bank_of(tag)
             for c in range(D_TILES):
                 nc.tensor.transpose(
                     t_banks[i][:, c * P : (c + 1) * P], t_rows[:, c, i * P : (i + 1) * P], ident[:]
                 )
 
-        ctx.enter_context(tc.manual_schedule())
-        transpose_h(0)
-        quantise_h(0)
-        transpose_w1(0)
-        quantise_w1(0)
-        transpose_w1(1)
-        prepare_biases()
-        quantise_w1(1)
-
-        first_matmul(0)
-        transpose_w1(2)
-        transpose_w1(3)
-        regroup(0)
-        quantise_w1(2)
-        quantise_a(0)
-        quantise_w1(3)
-
-        first_matmul(1)
-        transpose_h(1)
-        for c in range(D_TILES):
-            transpose_w2_rows(c)
-        regroup(1)
-        quantise_h(1)
-        quantise_a(1)
-        for g in range(GROUPS):
-            quantise_w2(g)
-
-        for unit in range(LAG, UNITS):
-            first_matmul(unit)
-            second_matmul(unit - LAG)
-            regroup(unit)
-            if unit - LAG == GROUPS - 1:
-                for c in range(D_TILES):
-                    add_residual(0, c)
-            quantise_a(unit)
-        for c in range(D_TILES):
-            sum_squares(0, c)
-        for unit in range(UNITS - LAG, UNITS):
-            second_matmul(unit)
-        for i in range(HALF_TILES):
-            transpose_back(i)
-        for c in range(D_TILES):
-            add_residual(1, c)
-            sum_squares(1, c)
-
-        moments_ps = new_bank()
-        nc.tensor.matmul(
-            out=moments_ps[:, 0 : 4 * D_TILES],
-            lhsT=mean_w[:],
-            rhs=partial[:].rearrange("p s x -> p (s x)"),
-            start=True,
-            stop=True,
-        )
-        for i in range(HALF_TILES, TOKEN_TILES):
-            transpose_back(i)
-        moments = keep.tile([P, 2], F32)
-        nc.vector.tensor_reduce(
-            out=moments[:],
-            in_=moments_ps[:, 0 : 4 * D_TILES].rearrange("p (s x) -> p s x", s=2),
-            axis=AXIS.X,
-            op=ALU.add,
-        )
-        mean = moments[:, 0:1]
-        neg_var = keep.tile([P, 1], F32)
-        nc.vector.scalar_tensor_tensor(
-            out=neg_var[:], in0=mean, scalar=mean, in1=moments[:, 1:2], op0=ALU.mult, op1=ALU.subtract
-        )
-        std = keep.tile([P, 1], F32)
-        nc.scalar.activation(out=std[:], in_=neg_var[:], func=ACT.Sqrt, scale=-1.0, bias=eps_col[:])
-        rstd = keep.tile([P, 1], F32)
-        nc.vector.reciprocal(out=rstd[:], in_=std[:])
-        shift = keep.tile([P, 1], F32)
-        nc.vector.scalar_tensor_tensor(
-            out=shift[:], in0=mean, scalar=-1.0, in1=rstd[:], op0=ALU.mult, op1=ALU.mult
-        )
-        for i in range(TOKEN_TILES):
+        def normalise(i, engine):
             from_bank = t_banks[i][:].rearrange("r (k e p) -> r k p e", k=2, e=PAIR)
             to_sbuf = y_sb[:, i, :].rearrange("r (k p e) -> r k p e", k=2, e=PAIR)
-            if i % 2 == 0:
+            if engine == "v":
                 nc.vector.tensor_scalar(
                     out=to_sbuf, in0=from_bank, scalar1=mean, scalar2=rstd[:], op0=ALU.subtract, op1=ALU.mult
                 )
-                nc.sync.dma_start(out=out_view[:, i, :], in_=y_sb[:, i, :])
             else:
                 nc.scalar.activation(
                     out=to_sbuf, in_=from_bank, func=ACT.Identity, scale=rstd[:], bias=shift[:]
                 )
-                nc.scalar.dma_start(out=out_view[:, i, :], in_=y_sb[:, i, :])
+            nc.sync.dma_start(out=out_view[:, i, :], in_=y_sb[:, i, :])
+
+        ctx.enter_context(tc.manual_schedule())
+
+        def quarter_matmul(quarter, u):
+            for c in range(D_TILES):
+                second_pass(quarter, u - 4, c, quarter * 256, 256, bank_of(("sum%d" if quarter == 2 else "work%d") % c) if u == 4 else None)
+        def regroup_unit(u):
+            for first in (0, 256):
+                regroup(u, first, 256)
+        def quantise_unit(u):
+            for first in (0, 256):
+                quantise_a(u, first, 256)
+        transpose_h(0, "v", bank_of("sum0"))
+        transpose_h(1, "v", bank_of("sum1"))
+        transpose_w1(0, "s", bank_of("sum2"))
+        transpose_w1(1, "s", bank_of("sum3"))
+        quantise_h(0)
+        quantise_h(1)
+        prepare_biases(new_bank())
+        quantise_w1(0)
+        transpose_w1(2, "v")
+        quantise_w1(1)
+        transpose_w1(3, "s")
+        start_unit(0)
+        s_route(0, (0, 1, 2, 3))
+        transpose_w2(0, 0, "v", bank_of("sum0"))
+        quantise_w1(2)
+        transpose_w2(0, 1, "v", bank_of("sum1"))
+        transpose_w1(4, "s", bank_of("sum2"))
+        transpose_w1(5, "s", bank_of("sum3"))
+        quantise_w1(3)
+        quantise_w2(0)
+        for u in (1, 2, 3):
+            start_unit(u)
+            s_route(u, (0, 1, 2, 3))
+            if u >= 2:
+                second_matmul(u - 2)
+            if u == 3:
+                quantise_h(2)
+                quantise_h(3)
+            regroup_unit(u - 1)
+            if u < 3:
+                quantise_w1(2 * u + 2)
+                quantise_w1(2 * u + 3)
+            transpose_w2(u, 0, "v")
+            transpose_w2(u, 1, "s")
+            if u + 2 < 4:
+                transpose_w1(2 * u + 4, "s")
+                transpose_w1(2 * u + 5, "s")
+            if u == 2:
+                transpose_h(2, "s")
+                transpose_h(3, "s")
+            quantise_unit(u - 1)
+            quantise_w2(u)
+        for u in (4, 5, 6, 7):
+            start_unit(u)
+            if u == 7:
+                s_route(u, (0, 1, 2, 3), 0, 256)
+                s_route(u, (0, 1, 2, 3), 256, 256)
+            else:
+                s_route(u, (0, 1, 2, 3))
+            if u < 6:
+                second_matmul(u - 2)
+            regroup_unit(u - 1)
+            if u == 6:
+                for c in range(D_TILES):
+                    add_residual(0, c, 0, 512, c)
+            if u == 7:
+                quarter_matmul(2, 4)
+                quarter_matmul(2, 5)
+            quantise_unit(u - 1)
+        quarter_matmul(2, 6)
+        for c in range(D_TILES):
+            sum_squares(c, 0, 512, c)
+        regroup(7, 0, 256)
+        quantise_a(7, 0, 256)
+        regroup(7, 256, 256)
+        quantise_a(7, 256, 256)
+        for u in (4, 5, 6):
+            quarter_matmul(3, u)
+        quarter_matmul(2, 7)
+        quarter_matmul(3, 7)
+        for c in range(D_TILES):
+            add_residual(2, c, 512, 256, 4 + c)
+            sum_squares(c, 512, 256, 4 + c)
+        for c in range(D_TILES):
+            add_residual(3, c, 768, 256, 8 + c)
+            sum_squares(c, 768, 256, 8 + c)
+
+        moments_ps = bank_of("sum0")
+        nc.tensor.matmul(out=moments_ps[:, 0:2 * COLS], lhsT=mean_w[:], rhs=partial[:].rearrange("p s x -> p (s x)"), start=True, stop=True)
+        for i in range(3):
+            transpose_back(i, "sum%d" % (i + 1))
+        for i in range(3, 7):
+            transpose_back(i, "work%d" % (i - 3))
+        moments = keep.tile([P, 2], F32)
+        nc.vector.tensor_reduce(out=moments[:], in_=moments_ps[:, 0:2 * COLS].rearrange("p (s x) -> p s x", s=2), axis=AXIS.X, op=ALU.add)
+        mean = moments[:, 0:1]
+        neg_var = keep.tile([P, 1], F32)
+        nc.vector.scalar_tensor_tensor(out=neg_var[:], in0=mean, scalar=mean, in1=moments[:, 1:2], op0=ALU.mult, op1=ALU.subtract)
+        rstd = keep.tile([P, 1], F32)
+        nc.scalar.activation(out=rstd[:], in_=neg_var[:], func=ACT.Abs_reciprocal_sqrt, scale=-1.0, bias=eps_col[:])
+        shift = keep.tile([P, 1], F32)
+        nc.vector.scalar_tensor_tensor(out=shift[:], in0=mean, scalar=-1.0, in1=rstd[:], op0=ALU.mult, op1=ALU.mult)
+        transpose_back(7, "sum0")
+        for i in range(TOKEN_TILES):
+            normalise(i, "vs"[i % 2])

@@ -33,7 +33,7 @@ B2_ROWS = D // (PAIR * P)
 HALF_TOKENS = TOKENS // 2
 BLOCK = P
 
-RV = ((0, 1),)
+RV = ((0, 1, 0),)
 
 FLOPS = 2 * TOKENS * D * F * 2
 
@@ -76,6 +76,7 @@ def tile_decoderblock_pb_kernel(tc, h2, w_ff1, b_ff1, w_ff2, b_ff2, out):
         COLS = 16
         partial = keep.tile([P, 2, COLS], F32)
 
+        idle = keep.tile([P, BANK], BF16)
         ident = keep.tile([P, P], F32)
         mean_w = keep.tile([P, P], F32)
         eps_col = keep.tile([P, 1], F32)
@@ -84,6 +85,7 @@ def tile_decoderblock_pb_kernel(tc, h2, w_ff1, b_ff1, w_ff2, b_ff2, out):
         bias_words = keep.tile([P, B1_ROWS + B2_ROWS], F32)
         bias_col = keep.tile([P, F_TILES + D_TILES], F32)
 
+        nc.vector.memset(idle[:], 0.0)
         nc.vector.memset(bias_rows[:], 0.0)
         nc.vector.memset(eps_col[:], EPS)
         nc.vector.memset(mean_w[:], 1.0 / (TOKENS * D))
@@ -152,6 +154,10 @@ def tile_decoderblock_pb_kernel(tc, h2, w_ff1, b_ff1, w_ff2, b_ff2, out):
                 nc.vector.tensor_copy(out=out_, in_=in_)
             else:
                 nc.scalar.copy(out=out_, in_=in_)
+
+        def warm_up(passes, bank):
+            for n in range(passes):
+                nc.tensor.matmul(out=bank[:], lhsT=idle[:, 0:P], rhs=idle[:], start=True, stop=True)
 
         def transpose_h(pair, engine, bank=None):
             i0 = 2 * pair
@@ -234,7 +240,7 @@ def tile_decoderblock_pb_kernel(tc, h2, w_ff1, b_ff1, w_ff2, b_ff2, out):
         def relu_rows(unit, v, first, width, bank, col):
             half, g = divmod(unit, GROUPS)
             j = PACK * g + v
-            if (unit, v) in RV:
+            if (unit, v, first) in RV:
                 nc.vector.tensor_scalar(
                     out=a_rows[unit][:, v, first : first + width],
                     in0=bank[:, col : col + width],
@@ -368,8 +374,10 @@ def tile_decoderblock_pb_kernel(tc, h2, w_ff1, b_ff1, w_ff2, b_ff2, out):
         def quantise_unit(u):
             for first in (0, 256):
                 quantise_a(u, first, 256)
+        warm_up(5, bank_of("work3"))
         transpose_h(0, "v", bank_of("sum0"))
         transpose_h(1, "v", bank_of("sum1"))
+        warm_up(2, bank_of("work3"))
         transpose_w1(0, "s", bank_of("sum2"))
         transpose_w1(1, "s", bank_of("sum3"))
         quantise_h(0)
@@ -426,16 +434,20 @@ def tile_decoderblock_pb_kernel(tc, h2, w_ff1, b_ff1, w_ff2, b_ff2, out):
             if u == 7:
                 quarter_matmul(2, 4)
                 quarter_matmul(2, 5)
+                quarter_matmul(3, 4)
+                quarter_matmul(3, 5)
             quantise_unit(u - 1)
         quarter_matmul(2, 6)
+        nc.scalar.copy(
+            out=a_grouped[7][:, 256:512, :].rearrange("p (c n) v -> p c v n", n=4),
+            in_=a_rows[7][:, :, 256:512].rearrange("p v (c n) -> p c v n", n=4),
+        )
         for c in range(D_TILES):
             sum_squares(c, 0, 512, c)
         regroup(7, 0, 256)
         quantise_a(7, 0, 256)
-        regroup(7, 256, 256)
         quantise_a(7, 256, 256)
-        for u in (4, 5, 6):
-            quarter_matmul(3, u)
+        quarter_matmul(3, 6)
         quarter_matmul(2, 7)
         quarter_matmul(3, 7)
         for c in range(D_TILES):
@@ -445,12 +457,12 @@ def tile_decoderblock_pb_kernel(tc, h2, w_ff1, b_ff1, w_ff2, b_ff2, out):
             add_residual(3, c, 768, 256, 8 + c)
             sum_squares(c, 768, 256, 8 + c)
 
-        moments_ps = bank_of("sum0")
-        nc.tensor.matmul(out=moments_ps[:, 0:2 * COLS], lhsT=mean_w[:], rhs=partial[:].rearrange("p s x -> p (s x)"), start=True, stop=True)
-        for i in range(3):
-            transpose_back(i, "sum%d" % (i + 1))
-        for i in range(3, 7):
+        for i in range(4):
+            transpose_back(i, "sum%d" % i)
+        for i in range(4, 7):
             transpose_back(i, "work%d" % (i - 3))
+        moments_ps = bank_of("work0")
+        nc.tensor.matmul(out=moments_ps[:, 0:2 * COLS], lhsT=mean_w[:], rhs=partial[:].rearrange("p s x -> p (s x)"), start=True, stop=True)
         moments = keep.tile([P, 2], F32)
         nc.vector.tensor_reduce(out=moments[:], in_=moments_ps[:, 0:2 * COLS].rearrange("p (s x) -> p s x", s=2), axis=AXIS.X, op=ALU.add)
         mean = moments[:, 0:1]
@@ -460,6 +472,6 @@ def tile_decoderblock_pb_kernel(tc, h2, w_ff1, b_ff1, w_ff2, b_ff2, out):
         nc.scalar.activation(out=rstd[:], in_=neg_var[:], func=ACT.Abs_reciprocal_sqrt, scale=-1.0, bias=eps_col[:])
         shift = keep.tile([P, 1], F32)
         nc.vector.scalar_tensor_tensor(out=shift[:], in0=mean, scalar=-1.0, in1=rstd[:], op0=ALU.mult, op1=ALU.mult)
-        transpose_back(7, "sum0")
+        transpose_back(7, "work0")
         for i in range(TOKEN_TILES):
             normalise(i, "vs"[i % 2])

@@ -76,7 +76,6 @@ def tile_decoderblock_pb_kernel(tc, h2, w_ff1, b_ff1, w_ff2, b_ff2, out):
         COLS = 16
         partial = keep.tile([P, 2, COLS], F32)
 
-        idle = keep.tile([P, BANK], BF16)
         ident = keep.tile([P, P], F32)
         mean_w = keep.tile([P, P], F32)
         eps_col = keep.tile([P, 1], F32)
@@ -85,7 +84,6 @@ def tile_decoderblock_pb_kernel(tc, h2, w_ff1, b_ff1, w_ff2, b_ff2, out):
         bias_words = keep.tile([P, B1_ROWS + B2_ROWS], F32)
         bias_col = keep.tile([P, F_TILES + D_TILES], F32)
 
-        nc.vector.memset(idle[:], 0.0)
         nc.vector.memset(bias_rows[:], 0.0)
         nc.vector.memset(eps_col[:], EPS)
         nc.vector.memset(mean_w[:], 1.0 / (TOKENS * D))
@@ -154,10 +152,6 @@ def tile_decoderblock_pb_kernel(tc, h2, w_ff1, b_ff1, w_ff2, b_ff2, out):
                 nc.vector.tensor_copy(out=out_, in_=in_)
             else:
                 nc.scalar.copy(out=out_, in_=in_)
-
-        def warm_up(passes, bank):
-            for n in range(passes):
-                nc.tensor.matmul(out=bank[:], lhsT=idle[:, 0:P], rhs=idle[:], start=True, stop=True)
 
         def transpose_h(pair, engine, bank=None):
             i0 = 2 * pair
@@ -350,18 +344,18 @@ def tile_decoderblock_pb_kernel(tc, h2, w_ff1, b_ff1, w_ff2, b_ff2, out):
                     t_banks[i][:, c * P : (c + 1) * P], t_rows[:, c, i * P : (i + 1) * P], ident[:]
                 )
 
-        def normalise(i, engine):
-            from_bank = t_banks[i][:].rearrange("r (k e p) -> r k p e", k=2, e=PAIR)
-            to_sbuf = y_sb[:, i, :].rearrange("r (k p e) -> r k p e", k=2, e=PAIR)
+        def normalise(i, engine, half=None):
+            halves = slice(0, PAIR) if half is None else slice(half, half + 1)
+            from_bank = t_banks[i][:].rearrange("r (k e p) -> r k p e", k=2, e=PAIR)[:, halves]
+            to_sbuf = y_sb[:, i, :].rearrange("r (k p e) -> r k p e", k=2, e=PAIR)[:, halves]
             if engine == "v":
                 nc.vector.tensor_scalar(
-                    out=to_sbuf, in0=from_bank, scalar1=mean, scalar2=rstd[:], op0=ALU.subtract, op1=ALU.mult
+                    out=to_sbuf, in0=from_bank, scalar1=mean[:], scalar2=rstd[:], op0=ALU.subtract, op1=ALU.mult
                 )
             else:
                 nc.scalar.activation(
                     out=to_sbuf, in_=from_bank, func=ACT.Identity, scale=rstd[:], bias=shift[:]
                 )
-            nc.sync.dma_start(out=out_view[:, i, :], in_=y_sb[:, i, :])
 
         ctx.enter_context(tc.manual_schedule())
 
@@ -374,10 +368,8 @@ def tile_decoderblock_pb_kernel(tc, h2, w_ff1, b_ff1, w_ff2, b_ff2, out):
         def quantise_unit(u):
             for first in (0, 256):
                 quantise_a(u, first, 256)
-        warm_up(5, bank_of("work3"))
         transpose_h(0, "v", bank_of("sum0"))
         transpose_h(1, "v", bank_of("sum1"))
-        warm_up(2, bank_of("work3"))
         transpose_w1(0, "s", bank_of("sum2"))
         transpose_w1(1, "s", bank_of("sum3"))
         quantise_h(0)
@@ -459,19 +451,33 @@ def tile_decoderblock_pb_kernel(tc, h2, w_ff1, b_ff1, w_ff2, b_ff2, out):
 
         for i in range(4):
             transpose_back(i, "sum%d" % i)
-        for i in range(4, 7):
-            transpose_back(i, "work%d" % (i - 3))
-        moments_ps = bank_of("work0")
-        nc.tensor.matmul(out=moments_ps[:, 0:2 * COLS], lhsT=mean_w[:], rhs=partial[:].rearrange("p s x -> p (s x)"), start=True, stop=True)
-        moments = keep.tile([P, 2], F32)
-        nc.vector.tensor_reduce(out=moments[:], in_=moments_ps[:, 0:2 * COLS].rearrange("p (s x) -> p s x", s=2), axis=AXIS.X, op=ALU.add)
-        mean = moments[:, 0:1]
-        neg_var = keep.tile([P, 1], F32)
-        nc.vector.scalar_tensor_tensor(out=neg_var[:], in0=mean, scalar=mean, in1=moments[:, 1:2], op0=ALU.mult, op1=ALU.subtract)
+        transpose_back(4, "work0")
+        transpose_back(5, "work1")
+        mean_ps = bank_of("work2")
+        nc.tensor.matmul(out=mean_ps[:, 0:COLS], lhsT=mean_w[:], rhs=partial[:, 0, :], start=True, stop=True)
+        msq_ps = bank_of("work3")
+        nc.tensor.matmul(out=msq_ps[:, 0:COLS], lhsT=mean_w[:], rhs=partial[:, 1, :], start=True, stop=True)
+        mean = keep.tile([P, 1], F32)
+        nc.vector.tensor_reduce(out=mean[:], in_=mean_ps[:, 0:COLS], axis=AXIS.X, op=ALU.add)
+        neg_mean = keep.tile([P, 1], F32)
+        nc.vector.tensor_scalar(out=neg_mean[:], in0=mean[:], scalar1=-1.0, scalar2=None, op0=ALU.mult)
+        eps_less = keep.tile([P, 1], F32)
+        nc.vector.scalar_tensor_tensor(out=eps_less[:], in0=mean[:], scalar=neg_mean[:], in1=eps_col[:], op0=ALU.mult, op1=ALU.add)
+        msq_cols = keep.tile([P, COLS], F32)
+        msq = keep.tile([P, 1], F32)
+        nc.scalar.activation(out=msq_cols[:], in_=msq_ps[:, 0:COLS], func=ACT.Copy, accum_out=msq[:])
         rstd = keep.tile([P, 1], F32)
-        nc.scalar.activation(out=rstd[:], in_=neg_var[:], func=ACT.Abs_reciprocal_sqrt, scale=-1.0, bias=eps_col[:])
+        nc.scalar.activation(out=rstd[:], in_=msq[:], func=ACT.Abs_reciprocal_sqrt, scale=1.0, bias=eps_less[:])
         shift = keep.tile([P, 1], F32)
-        nc.vector.scalar_tensor_tensor(out=shift[:], in0=mean, scalar=-1.0, in1=rstd[:], op0=ALU.mult, op1=ALU.mult)
-        transpose_back(7, "work0")
-        for i in range(TOKEN_TILES):
-            normalise(i, "vs"[i % 2])
+        nc.scalar.activation(out=shift[:], in_=rstd[:], func=ACT.Copy, scale=neg_mean[:])
+        transpose_back(6, "work2")
+        transpose_back(7, "work3")
+        for half in range(2):
+            normalise(0, "v", half)
+            nc.sync.dma_start(out=out_view[:, 0, half * 256 : (half + 1) * 256], in_=y_sb[:, 0, half * 256 : (half + 1) * 256])
+        for i in range(1, TOKEN_TILES):
+            normalise(i, "sv"[i % 2] if i > 1 else "s")
+            if i == 1:
+                nc.sync.dma_start(out=out_view[:, i, :], in_=y_sb[:, i, :])
+            elif i % 2 == 1:
+                nc.sync.dma_start(out=out_view[:, i - 1 : i + 1, :], in_=y_sb[:, i - 1 : i + 1, :])

@@ -33,8 +33,6 @@ B2_ROWS = D // (PAIR * P)
 HALF_TOKENS = TOKENS // 2
 BLOCK = P
 
-RV = ((0, 1, 0),)
-
 FLOPS = 2 * TOKENS * D * F * 2
 
 
@@ -76,6 +74,7 @@ def tile_decoderblock_pb_kernel(tc, h2, w_ff1, b_ff1, w_ff2, b_ff2, out):
         COLS = 16
         partial = keep.tile([P, 2, COLS], F32)
 
+        idle = keep.tile([P, BANK // 2], BF16)
         ident = keep.tile([P, P], F32)
         mean_w = keep.tile([P, P], F32)
         eps_col = keep.tile([P, 1], F32)
@@ -84,6 +83,7 @@ def tile_decoderblock_pb_kernel(tc, h2, w_ff1, b_ff1, w_ff2, b_ff2, out):
         bias_words = keep.tile([P, B1_ROWS + B2_ROWS], F32)
         bias_col = keep.tile([P, F_TILES + D_TILES], F32)
 
+        nc.vector.memset(idle[:], 1.0)
         nc.vector.memset(bias_rows[:], 0.0)
         nc.vector.memset(eps_col[:], EPS)
         nc.vector.memset(mean_w[:], 1.0 / (TOKENS * D))
@@ -153,6 +153,10 @@ def tile_decoderblock_pb_kernel(tc, h2, w_ff1, b_ff1, w_ff2, b_ff2, out):
             else:
                 nc.scalar.copy(out=out_, in_=in_)
 
+        def warm_up(passes, bank):
+            for n in range(passes):
+                nc.tensor.matmul(out=bank[:, 0 : BANK // 2], lhsT=idle[:, 0:P], rhs=idle[:], start=True, stop=True)
+
         def transpose_h(pair, engine, bank=None):
             i0 = 2 * pair
             if bank is None:
@@ -164,13 +168,10 @@ def tile_decoderblock_pb_kernel(tc, h2, w_ff1, b_ff1, w_ff2, b_ff2, out):
             cols = slice(i0 * P * PACK, (i0 + 2) * P * PACK)
             copy_out(engine, as_words(h_grouped[:, cols]), interleaved(bank))
 
-        def quantise_h(pair):
+        def quantise_h(pair, banks=1):
             first = pair * bank_cols
-            quantise(
-                h_grouped[:, first * PACK : (first + bank_cols) * PACK],
-                h_codes[:, first : first + bank_cols],
-                h_scales[:, first : first + bank_cols],
-            )
+            last = first + banks * bank_cols
+            quantise(h_grouped[:, first * PACK : last * PACK], h_codes[:, first:last], h_scales[:, first:last])
 
         def prepare_biases(bank):
             transpose_words(bank, 0, bias_rows[:])
@@ -187,13 +188,10 @@ def tile_decoderblock_pb_kernel(tc, h2, w_ff1, b_ff1, w_ff2, b_ff2, out):
             cols = slice(q * 2 * P * PACK, (q + 1) * 2 * P * PACK)
             copy_out(engine, as_words(w1_grouped[:, cols]), interleaved(bank))
 
-        def quantise_w1(q):
+        def quantise_w1(q, banks=1):
             first = q * bank_cols
-            quantise(
-                w1_grouped[:, first * PACK : (first + bank_cols) * PACK],
-                w1_codes[:, first : first + bank_cols],
-                w1_scales[:, first : first + bank_cols],
-            )
+            last = first + banks * bank_cols
+            quantise(w1_grouped[:, first * PACK : last * PACK], w1_codes[:, first:last], w1_scales[:, first:last])
 
         def transpose_w2(g, k, engine, bank=None):
             if bank is None:
@@ -234,16 +232,6 @@ def tile_decoderblock_pb_kernel(tc, h2, w_ff1, b_ff1, w_ff2, b_ff2, out):
         def relu_rows(unit, v, first, width, bank, col):
             half, g = divmod(unit, GROUPS)
             j = PACK * g + v
-            if (unit, v, first) in RV:
-                nc.vector.tensor_scalar(
-                    out=a_rows[unit][:, v, first : first + width],
-                    in0=bank[:, col : col + width],
-                    scalar1=bias_col[:, j : j + 1],
-                    scalar2=0.0,
-                    op0=ALU.add,
-                    op1=ALU.max,
-                )
-                return
             nc.scalar.activation(
                 out=a_rows[unit][:, v, first : first + width],
                 in_=bank[:, col : col + width],
@@ -260,23 +248,6 @@ def tile_decoderblock_pb_kernel(tc, h2, w_ff1, b_ff1, w_ff2, b_ff2, out):
                     first_pass(unit, v0 + x, first, width, bank, x * width)
                 for x in range(per_bank):
                     relu_rows(unit, v0 + x, first, width, bank, x * width)
-
-        def v_pass(unit, block):
-            half, g = divmod(unit, GROUPS)
-            bank = new_bank()
-            for v in range(PACK):
-                first_pass(unit, v, block * BLOCK, BLOCK, bank, v * BLOCK)
-            bias = bias_col[:, PACK * g : PACK * (g + 1)].unsqueeze(1).to_broadcast([P, BLOCK, PACK])
-            nc.vector.tensor_tensor(
-                out=a_grouped[unit][:, block * BLOCK : (block + 1) * BLOCK, :],
-                in0=bank[:].rearrange("p (v n) -> p n v", v=PACK),
-                in1=bias,
-                op=ALU.add,
-            )
-
-        def v_relu(unit, b0, b1):
-            part = a_grouped[unit][:, b0 * BLOCK : b1 * BLOCK, :].rearrange("p n v -> p (n v)")
-            nc.vector.tensor_scalar_max(out=part, in0=part, scalar1=0.0)
 
         def regroup(unit, first, width):
             tok = slice(first, first + width)
@@ -368,8 +339,10 @@ def tile_decoderblock_pb_kernel(tc, h2, w_ff1, b_ff1, w_ff2, b_ff2, out):
         def quantise_unit(u):
             for first in (0, 256):
                 quantise_a(u, first, 256)
+        warm_up(8, bank_of("work3"))
         transpose_h(0, "v", bank_of("sum0"))
         transpose_h(1, "v", bank_of("sum1"))
+        warm_up(4, bank_of("work3"))
         transpose_w1(0, "s", bank_of("sum2"))
         transpose_w1(1, "s", bank_of("sum3"))
         quantise_h(0)
@@ -379,14 +352,15 @@ def tile_decoderblock_pb_kernel(tc, h2, w_ff1, b_ff1, w_ff2, b_ff2, out):
         transpose_w1(2, "v")
         quantise_w1(1)
         transpose_w1(3, "s")
-        start_unit(0)
-        s_route(0, (0, 1, 2, 3))
-        transpose_w2(0, 0, "v", bank_of("sum0"))
         quantise_w1(2)
+        quantise_w1(3)
+        start_unit(0)
+        s_route(0, (0, 1))
+        transpose_w2(0, 0, "v", bank_of("sum0"))
+        s_route(0, (2, 3))
         transpose_w2(0, 1, "v", bank_of("sum1"))
         transpose_w1(4, "s", bank_of("sum2"))
         transpose_w1(5, "s", bank_of("sum3"))
-        quantise_w1(3)
         quantise_w2(0)
         for u in (1, 2, 3):
             start_unit(u)

@@ -193,14 +193,23 @@ def tile_decoderblock_pb_kernel(tc, h2, w_ff1, b_ff1, w_ff2, b_ff2, out):
             last = first + banks * bank_cols
             quantise(w1_grouped[:, first * PACK : last * PACK], w1_codes[:, first:last], w1_scales[:, first:last])
 
-        def transpose_w2(g, k, engine, bank=None):
+        w2_banks = {}
+
+        def turn_w2(g, k, bank=None):
             if bank is None:
                 bank = new_bank()
             for e in range(PAIR):
                 for half in range(PAIR):
                     transpose_words(bank, 2 * e + half, w2_sb[:, g, k, e, half * PAIR * P : (half + 1) * PAIR * P])
+            w2_banks[g, k] = bank
+
+        def take_w2(g, k, engine):
             first = (g * D + k * bank_cols) * PACK
-            copy_out(engine, as_words(w2_grouped[:, first : first + bank_cols * PACK]), interleaved(bank))
+            copy_out(engine, as_words(w2_grouped[:, first : first + bank_cols * PACK]), interleaved(w2_banks[g, k]))
+
+        def transpose_w2(g, k, engine, bank=None):
+            turn_w2(g, k, bank)
+            take_w2(g, k, engine)
 
         def quantise_w2(g):
             quantise(
@@ -368,21 +377,22 @@ def tile_decoderblock_pb_kernel(tc, h2, w_ff1, b_ff1, w_ff2, b_ff2, out):
             if u >= 2:
                 second_matmul(u - 2)
             if u == 3:
-                quantise_h(2)
-                quantise_h(3)
-            regroup_unit(u - 1)
+                quantise_h(2, 2)
+            regroup(u - 1, 0, 512)
             if u < 3:
-                quantise_w1(2 * u + 2)
-                quantise_w1(2 * u + 3)
-            transpose_w2(u, 0, "v")
-            transpose_w2(u, 1, "s")
+                quantise_w1(2 * u + 2, 2)
+            spare = [bank_of("sum%d" % c) for c in range(4)] if u == 1 else [None] * 4
+            transpose_w2(u, 0, "v", spare[0])
+            transpose_w2(u, 1, "s", spare[1])
             if u + 2 < 4:
-                transpose_w1(2 * u + 4, "s")
-                transpose_w1(2 * u + 5, "s")
+                if u == 1:
+                    warm_up(4, spare[2])
+                transpose_w1(2 * u + 4, "s", spare[2])
+                transpose_w1(2 * u + 5, "s", spare[3])
             if u == 2:
                 transpose_h(2, "s")
                 transpose_h(3, "s")
-            quantise_unit(u - 1)
+            quantise_a(u - 1, 0, 512)
             quantise_w2(u)
         for u in (4, 5, 6, 7):
             start_unit(u)
@@ -405,12 +415,12 @@ def tile_decoderblock_pb_kernel(tc, h2, w_ff1, b_ff1, w_ff2, b_ff2, out):
             quantise_unit(u - 1)
         quarter_matmul(2, 6)
         nc.scalar.copy(
-            out=a_grouped[7][:, 256:512, :].rearrange("p (c n) v -> p c v n", n=4),
-            in_=a_rows[7][:, :, 256:512].rearrange("p v (c n) -> p c v n", n=4),
+            out=a_grouped[7][:, 0:256, :].rearrange("p (c n) v -> p c v n", n=4),
+            in_=a_rows[7][:, :, 0:256].rearrange("p v (c n) -> p c v n", n=4),
         )
         for c in range(D_TILES):
             sum_squares(c, 0, 512, c)
-        regroup(7, 0, 256)
+        regroup(7, 256, 256)
         quantise_a(7, 0, 256)
         quantise_a(7, 256, 256)
         quarter_matmul(3, 6)
@@ -426,7 +436,6 @@ def tile_decoderblock_pb_kernel(tc, h2, w_ff1, b_ff1, w_ff2, b_ff2, out):
         for i in range(4):
             transpose_back(i, "sum%d" % i)
         transpose_back(4, "work0")
-        transpose_back(5, "work1")
         mean_ps = bank_of("work2")
         nc.tensor.matmul(out=mean_ps[:, 0:COLS], lhsT=mean_w[:], rhs=partial[:, 0, :], start=True, stop=True)
         msq_ps = bank_of("work3")
@@ -444,6 +453,7 @@ def tile_decoderblock_pb_kernel(tc, h2, w_ff1, b_ff1, w_ff2, b_ff2, out):
         nc.scalar.activation(out=rstd[:], in_=msq[:], func=ACT.Abs_reciprocal_sqrt, scale=1.0, bias=eps_less[:])
         shift = keep.tile([P, 1], F32)
         nc.scalar.activation(out=shift[:], in_=rstd[:], func=ACT.Copy, scale=neg_mean[:])
+        transpose_back(5, "work1")
         transpose_back(6, "work2")
         transpose_back(7, "work3")
         for half in range(2):

@@ -294,11 +294,11 @@ def tile_decoderblock_pb_kernel(tc, h2, w_ff1, b_ff1, w_ff2, b_ff2, out):
 
         h_by_value = h_grouped[:].rearrange("p (n v) -> p n v", v=PACK)
 
-        def add_residual(key, c, first, width, col):
+        def add_residual(key, c, first, width, col, bank_col=0):
             tok = slice(first, first + width)
             nc.vector.scalar_tensor_tensor(
                 out=t_rows[:, c, tok],
-                in0=open_sums[key, c][:, 0:width],
+                in0=open_sums[key, c][:, bank_col : bank_col + width],
                 scalar=bias_col[:, F_TILES + c : F_TILES + c + 1],
                 in1=h_by_value[:, tok, c],
                 op0=ALU.add,
@@ -306,11 +306,11 @@ def tile_decoderblock_pb_kernel(tc, h2, w_ff1, b_ff1, w_ff2, b_ff2, out):
                 accum_out=partial[:, 0, col : col + 1],
             )
 
-        def sum_squares(c, first, width, col):
+        def sum_squares(c, first, width, col, tiles=1):
             tok = slice(first, first + width)
             nc.scalar.activation(
-                out=squares[:, c, tok],
-                in_=t_rows[:, c, tok],
+                out=squares[:, c : c + tiles, tok],
+                in_=t_rows[:, c : c + tiles, tok],
                 func=ACT.Square,
                 accum_out=partial[:, 1, col : col + 1],
             )
@@ -339,9 +339,9 @@ def tile_decoderblock_pb_kernel(tc, h2, w_ff1, b_ff1, w_ff2, b_ff2, out):
 
         ctx.enter_context(tc.manual_schedule())
 
-        def quarter_matmul(quarter, u):
-            for c in range(D_TILES):
-                second_pass(quarter, u - 4, c, quarter * 256, 256, bank_of(("sum%d" if quarter == 2 else "work%d") % c) if u == 4 else None)
+        def sums_of_second_half(u, tiles):
+            for c in tiles:
+                second_pass(1, u - 4, c, 512, 512, bank_of("sum%d" % c if c < 3 else "work0") if u == 4 else None)
         def regroup_unit(u):
             for first in (0, 256):
                 regroup(u, first, 256)
@@ -405,40 +405,35 @@ def tile_decoderblock_pb_kernel(tc, h2, w_ff1, b_ff1, w_ff2, b_ff2, out):
                 second_matmul(u - 2)
             regroup_unit(u - 1)
             if u == 6:
-                for c in range(D_TILES):
+                for c in range(3):
                     add_residual(0, c, 0, 512, c)
             if u == 7:
-                quarter_matmul(2, 4)
-                quarter_matmul(2, 5)
-                quarter_matmul(3, 4)
-                quarter_matmul(3, 5)
+                sums_of_second_half(4, range(3))
+                sums_of_second_half(5, range(3))
             quantise_unit(u - 1)
-        quarter_matmul(2, 6)
+        sums_of_second_half(6, range(3))
         nc.scalar.copy(
             out=a_grouped[7][:, 0:256, :].rearrange("p (c n) v -> p c v n", n=4),
             in_=a_rows[7][:, :, 0:256].rearrange("p v (c n) -> p c v n", n=4),
         )
-        for c in range(D_TILES):
-            sum_squares(c, 0, 512, c)
+        sum_squares(0, 0, 512, 0, 3)
+        for u in (4, 5, 6):
+            sums_of_second_half(u, (3,))
         regroup(7, 256, 256)
         quantise_a(7, 0, 256)
         quantise_a(7, 256, 256)
-        quarter_matmul(3, 6)
-        quarter_matmul(2, 7)
-        quarter_matmul(3, 7)
+        sums_of_second_half(7, range(D_TILES))
+        add_residual(0, 3, 0, 512, 3)
+        sum_squares(3, 0, 512, 3)
         for c in range(D_TILES):
-            add_residual(2, c, 512, 256, 4 + c)
-            sum_squares(c, 512, 256, 4 + c)
-        for c in range(D_TILES):
-            add_residual(3, c, 768, 256, 8 + c)
-            sum_squares(c, 768, 256, 8 + c)
-
-        for i in range(4):
-            transpose_back(i, "sum%d" % i)
-        transpose_back(4, "work0")
-        mean_ps = bank_of("work2")
+            add_residual(1, c, 512, 512, 4 + c)
+            sum_squares(c, 512, 512, 4 + c)
+        for i in range(3):
+            transpose_back(i, "work%d" % (i + 1))
+        transpose_back(3, "sum2")
+        mean_ps = bank_of("sum0")
         nc.tensor.matmul(out=mean_ps[:, 0:COLS], lhsT=mean_w[:], rhs=partial[:, 0, :], start=True, stop=True)
-        msq_ps = bank_of("work3")
+        msq_ps = bank_of("sum1")
         nc.tensor.matmul(out=msq_ps[:, 0:COLS], lhsT=mean_w[:], rhs=partial[:, 1, :], start=True, stop=True)
         mean = keep.tile([P, 1], F32)
         nc.vector.tensor_reduce(out=mean[:], in_=mean_ps[:, 0:COLS], axis=AXIS.X, op=ALU.add)
@@ -453,9 +448,10 @@ def tile_decoderblock_pb_kernel(tc, h2, w_ff1, b_ff1, w_ff2, b_ff2, out):
         nc.scalar.activation(out=rstd[:], in_=msq[:], func=ACT.Abs_reciprocal_sqrt, scale=1.0, bias=eps_less[:])
         shift = keep.tile([P, 1], F32)
         nc.scalar.activation(out=shift[:], in_=rstd[:], func=ACT.Copy, scale=neg_mean[:])
-        transpose_back(5, "work1")
-        transpose_back(6, "work2")
-        transpose_back(7, "work3")
+        transpose_back(4, "work0")
+        transpose_back(5, "sum3")
+        transpose_back(6, "sum0")
+        transpose_back(7, "sum1")
         for half in range(2):
             normalise(0, "v", half)
             nc.sync.dma_start(out=out_view[:, 0, half * 256 : (half + 1) * 256], in_=y_sb[:, 0, half * 256 : (half + 1) * 256])

from contextlib import ExitStack

import concourse.mybir as mybir
from concourse.masks import make_identity

F32 = mybir.dt.float32
BF16 = mybir.dt.bfloat16
U32 = mybir.dt.uint32
U8 = mybir.dt.uint8
FP8X4 = mybir.dt.float8_e4m3fn_x4
ACT = mybir.ActivationFunctionType
ALU = mybir.AluOpType
AXIS = mybir.AxisListType

P = 128
PACK = 4
K_PASS = P * PACK
BANK = 512
PAIR = 2

TOKENS = 1024
D = 512
F = 2048
EPS = 1e-5

TOKEN_TILES = TOKENS // P
GROUPS = F // K_PASS
F_TILES = F // P
D_TILES = D // P
B1_ROWS = F // (PAIR * P)
B2_ROWS = D // (PAIR * P)

HALF_TOKENS = TOKENS // 2
BLOCK = P

FLOPS = 2 * TOKENS * D * F * 2


def tile_decoderblock_pb_kernel(tc, h2, w_ff1, b_ff1, w_ff2, b_ff2, out):
    nc = tc.nc

    h_view = h2.flatten_outer_dims().rearrange("(r i) d -> r (i d)", i=TOKEN_TILES)
    out_view = out.flatten_outer_dims().rearrange("(r i) d -> r i d", i=TOKEN_TILES)
    w1_view = w_ff1.rearrange("(q p e) d -> p q (e d)", p=P, e=PAIR)
    w2_view = w_ff2.rearrange("(k p e) f -> p k e f", p=P, e=PAIR)
    b1_view = b_ff1.rearrange("(q x) -> q x", x=PAIR * P)
    b2_view = b_ff2.rearrange("(k x) -> k x", x=PAIR * P)

    with ExitStack() as ctx:
        keep = ctx.enter_context(tc.tile_pool(name="keep", bufs=1))
        ring = ctx.enter_context(tc.tile_pool(name="ring", bufs=3))
        psum = ctx.enter_context(tc.psum_pool(name="psum", bufs=1))

        h_sb = keep.tile([P, TOKEN_TILES * D], BF16)
        w1_sb = keep.tile([P, F_TILES * D], BF16)
        w2_sb = keep.tile([P, GROUPS, PAIR, PAIR, K_PASS], BF16)

        h_grouped = keep.tile([P, TOKENS * PACK], BF16, align_bytes=64)
        w1_grouped = keep.tile([P, F * PACK], BF16, align_bytes=64)
        w2_grouped = keep.tile([P, GROUPS * D * PACK], BF16, align_bytes=64)

        h_codes = keep.tile([P, TOKENS], U32, align_bytes=64)
        h_scales = keep.tile([P, TOKENS], U8, align_bytes=64)
        w1_codes = keep.tile([P, F], U32, align_bytes=64)
        w1_scales = keep.tile([P, F], U8, align_bytes=64)
        w2_codes = keep.tile([P, GROUPS, D], U32, align_bytes=64)
        w2_scales = keep.tile([P, GROUPS, D], U8, align_bytes=64)
        a_codes = keep.tile([P, GROUPS, TOKENS], U32, align_bytes=64)
        a_scales = keep.tile([P, GROUPS, TOKENS], U8, align_bytes=64)

        t_rows = keep.tile([P, D_TILES, TOKENS], F32)
        squares = keep.tile([P, D_TILES, TOKENS], BF16)
        y_sb = keep.tile([P, TOKEN_TILES, D], F32)
        COLS = 16
        partial = keep.tile([P, 2, COLS], F32)

        idle = keep.tile([P, BANK // 2], BF16)
        ident = keep.tile([P, P], F32)
        mean_w = keep.tile([P, P], F32)
        eps_col = keep.tile([P, 1], F32)
        warm = keep.tile([P, 1], F32)
        bias_rows = keep.tile([P, PAIR * P], BF16)
        bias_words = keep.tile([P, B1_ROWS + B2_ROWS], F32)
        bias_col = keep.tile([P, F_TILES + D_TILES], F32)

        nc.vector.memset(idle[:], 1.0)
        nc.vector.memset(bias_rows[:], 0.0)
        nc.vector.memset(eps_col[:], EPS)
        nc.vector.memset(mean_w[:], 1.0 / (TOKENS * D))
        nc.vector.memset(partial[:], 0.0)
        make_identity(nc, ident[:])

        nc.scalar.dma_start(out=bias_rows[0:B1_ROWS, :], in_=b1_view)
        nc.scalar.dma_start(out=bias_rows[B1_ROWS : B1_ROWS + B2_ROWS, :], in_=b2_view)
        nc.scalar.activation(out=warm[:], in_=eps_col[:], func=ACT.Abs_reciprocal_sqrt)

        def load_h(i0, n):
            nc.sync.dma_start(out=h_sb[:, i0 * D : (i0 + n) * D], in_=h_view[:, i0 * D : (i0 + n) * D])

        def load_w1(q):
            nc.sync.dma_start(out=w1_sb[:, q * PAIR * D : (q + 1) * PAIR * D], in_=w1_view[:, q, :])

        def load_w2(g):
            for k in range(PAIR):
                nc.sync.dma_start(
                    out=w2_sb[:, g, k, :, :], in_=w2_view[:, k, :, g * K_PASS : (g + 1) * K_PASS]
                )

        load_h(0, 1)
        load_h(1, 1)
        load_h(2, 2)
        load_w1(0)
        load_w1(1)
        load_w1(2)
        load_w1(3)
        load_w2(0)
        load_w1(4)
        load_w1(5)
        load_w2(1)
        load_w1(6)
        load_w1(7)
        load_w2(2)
        load_h(4, 4)
        load_w2(3)

        state = {"n": 0}

        def bank_of(tag):
            return psum.tile([P, BANK], F32, name=tag, tag=tag)

        def new_bank():
            n = state["n"]
            state["n"] = n + 1
            return bank_of("work%d" % (n % 4))

        def transpose_words(bank, slot, src):
            nc.tensor.transpose(bank[:, slot * P : (slot + 1) * P], src.bitcast(F32), ident[:])

        def interleaved(bank):
            return bank[:].rearrange("p (x k r) -> p x r k", x=2, k=PAIR)

        def as_words(grouped_cols):
            return grouped_cols.bitcast(F32).rearrange("p (x r k) -> p x r k", x=2, k=PAIR)

        def quantise(grouped_cols, codes, scales):
            nc.vector.quantize_mx(out=codes.bitcast(FP8X4), scales=scales, in_=grouped_cols)

        bank_cols = 2 * P

        def copy_out(engine, out_, in_):
            if engine == "v":
                nc.vector.tensor_copy(out=out_, in_=in_)
            else:
                nc.scalar.copy(out=out_, in_=in_)

        def warm_up(passes, bank):
            for n in range(passes):
                nc.tensor.matmul(out=bank[:, 0 : BANK // 2], lhsT=idle[:, 0:P], rhs=idle[:], start=True, stop=True)

        def transpose_h(pair, engine, bank=None):
            i0 = 2 * pair
            if bank is None:
                bank = new_bank()
            for x in range(2):
                for k in range(PAIR):
                    first = (i0 + x) * D + k * PAIR * P
                    transpose_words(bank, 2 * x + k, h_sb[:, first : first + PAIR * P])
            cols = slice(i0 * P * PACK, (i0 + 2) * P * PACK)
            copy_out(engine, as_words(h_grouped[:, cols]), interleaved(bank))

        def quantise_h(pair, banks=1):
            first = pair * bank_cols
            last = first + banks * bank_cols
            quantise(h_grouped[:, first * PACK : last * PACK], h_codes[:, first:last], h_scales[:, first:last])

        def prepare_biases(bank):
            transpose_words(bank, 0, bias_rows[:])
            nc.vector.tensor_copy(out=bias_words[:], in_=bank[:, 0 : B1_ROWS + B2_ROWS])
            nc.vector.tensor_copy(out=bias_col[:], in_=bias_words[:].bitcast(BF16))

        def transpose_w1(q, engine, bank=None):
            if bank is None:
                bank = new_bank()
            for e in range(PAIR):
                for k in range(PAIR):
                    first = (PAIR * q + e) * D + k * PAIR * P
                    transpose_words(bank, 2 * e + k, w1_sb[:, first : first + PAIR * P])
            cols = slice(q * 2 * P * PACK, (q + 1) * 2 * P * PACK)
            copy_out(engine, as_words(w1_grouped[:, cols]), interleaved(bank))

        def quantise_w1(q, banks=1):
            first = q * bank_cols
            last = first + banks * bank_cols
            quantise(w1_grouped[:, first * PACK : last * PACK], w1_codes[:, first:last], w1_scales[:, first:last])

        w2_banks = {}

        def turn_w2(g, k, bank=None):
            if bank is None:
                bank = new_bank()
            for e in range(PAIR):
                for half in range(PAIR):
                    transpose_words(bank, 2 * e + half, w2_sb[:, g, k, e, half * PAIR * P : (half + 1) * PAIR * P])
            w2_banks[g, k] = bank

        def take_w2(g, k, engine):
            first = (g * D + k * bank_cols) * PACK
            copy_out(engine, as_words(w2_grouped[:, first : first + bank_cols * PACK]), interleaved(w2_banks[g, k]))

        def transpose_w2(g, k, engine, bank=None):
            turn_w2(g, k, bank)
            take_w2(g, k, engine)

        def quantise_w2(g):
            quantise(
                w2_grouped[:, g * D * PACK : (g + 1) * D * PACK], w2_codes[:, g, :], w2_scales[:, g, :]
            )

        a_rows = {}
        a_grouped = {}
        open_sums = {}

        def start_unit(unit):
            a_rows[unit] = ring.tile([P, PACK, HALF_TOKENS], BF16, name="a_rows")
            a_grouped[unit] = ring.tile([P, HALF_TOKENS, PACK], BF16, name="a_grouped", align_bytes=64)

        def first_pass(unit, v, first, width, bank, col):
            half, g = divmod(unit, GROUPS)
            j = PACK * g + v
            t0 = half * HALF_TOKENS + first
            nc.tensor.matmul_mx(
                out=bank[:, col : col + width],
                lhsT=w1_codes[:, j * P : (j + 1) * P].bitcast(FP8X4),
                lhsT_scale=w1_scales[:, j * P : (j + 1) * P],
                rhs=h_codes[:, t0 : t0 + width].bitcast(FP8X4),
                rhs_scale=h_scales[:, t0 : t0 + width],
                start=True,
                stop=True,
            )

        def relu_rows(unit, v, first, width, bank, col):
            half, g = divmod(unit, GROUPS)
            j = PACK * g + v
            nc.scalar.activation(
                out=a_rows[unit][:, v, first : first + width],
                in_=bank[:, col : col + width],
                func=ACT.Relu,
                bias=bias_col[:, j : j + 1],
                scale=1.0,
            )

        def s_route(unit, values, first=0, width=HALF_TOKENS):
            per_bank = BANK // width
            for v0 in range(values[0], values[-1] + 1, per_bank):
                bank = new_bank()
                for x in range(per_bank):
                    first_pass(unit, v0 + x, first, width, bank, x * width)
                for x in range(per_bank):
                    relu_rows(unit, v0 + x, first, width, bank, x * width)

        def regroup(unit, first, width):
            tok = slice(first, first + width)
            nc.vector.tensor_copy(
                out=a_grouped[unit][:, tok, :].rearrange("p (c n) v -> p c v n", n=4),
                in_=a_rows[unit][:, :, tok].rearrange("p v (c n) -> p c v n", n=4),
            )

        def quantise_a(unit, first, width):
            half, g = divmod(unit, GROUPS)
            col = half * HALF_TOKENS + first
            quantise(
                a_grouped[unit][:, first : first + width, :].rearrange("p n v -> p (n v)"),
                a_codes[:, g, col : col + width],
                a_scales[:, g, col : col + width],
            )

        def second_pass(key, g, c, first, width, bank=None):
            if g == 0:
                open_sums[key, c] = bank_of("sum%d" % c) if bank is None else bank
            nc.tensor.matmul_mx(
                out=open_sums[key, c][:, 0:width],
                lhsT=w2_codes[:, g, c * P : (c + 1) * P].bitcast(FP8X4),
                lhsT_scale=w2_scales[:, g, c * P : (c + 1) * P],
                rhs=a_codes[:, g, first : first + width].bitcast(FP8X4),
                rhs_scale=a_scales[:, g, first : first + width],
                start=(g == 0),
                stop=(g == GROUPS - 1),
            )

        def second_matmul(unit):
            half, g = divmod(unit, GROUPS)
            for c in range(D_TILES):
                second_pass(half, g, c, half * HALF_TOKENS, HALF_TOKENS)

        h_by_value = h_grouped[:].rearrange("p (n v) -> p n v", v=PACK)

        def add_residual(key, c, first, width, col, bank_col=0):
            tok = slice(first, first + width)
            nc.vector.scalar_tensor_tensor(
                out=t_rows[:, c, tok],
                in0=open_sums[key, c][:, bank_col : bank_col + width],
                scalar=bias_col[:, F_TILES + c : F_TILES + c + 1],
                in1=h_by_value[:, tok, c],
                op0=ALU.add,
                op1=ALU.add,
                accum_out=partial[:, 0, col : col + 1],
            )

        def sum_squares(c, first, width, col, tiles=1):
            tok = slice(first, first + width)
            nc.scalar.activation(
                out=squares[:, c : c + tiles, tok],
                in_=t_rows[:, c : c + tiles, tok],
                func=ACT.Square,
                accum_out=partial[:, 1, col : col + 1],
            )

        t_banks = {}

        def transpose_back(i, tag):
            t_banks[i] = bank_of(tag)
            for c in range(D_TILES):
                nc.tensor.transpose(
                    t_banks[i][:, c * P : (c + 1) * P], t_rows[:, c, i * P : (i + 1) * P], ident[:]
                )

        def normalise(i, engine, half=None):
            halves = slice(0, PAIR) if half is None else slice(half, half + 1)
            from_bank = t_banks[i][:].rearrange("r (k e p) -> r k p e", k=2, e=PAIR)[:, halves]
            to_sbuf = y_sb[:, i, :].rearrange("r (k p e) -> r k p e", k=2, e=PAIR)[:, halves]
            if engine == "v":
                nc.vector.tensor_scalar(
                    out=to_sbuf, in0=from_bank, scalar1=mean[:], scalar2=rstd[:], op0=ALU.subtract, op1=ALU.mult
                )
            else:
                nc.scalar.activation(
                    out=to_sbuf, in_=from_bank, func=ACT.Identity, scale=rstd[:], bias=shift[:]
                )

        ctx.enter_context(tc.manual_schedule())

        def sums_of_second_half(u, tiles):
            for c in tiles:
                second_pass(1, u - 4, c, 512, 512, bank_of("sum%d" % c if c < 3 else "work0") if u == 4 else None)
        def regroup_unit(u):
            for first in (0, 256):
                regroup(u, first, 256)
        def quantise_unit(u):
            for first in (0, 256):
                quantise_a(u, first, 256)
        warm_up(8, bank_of("work3"))
        transpose_h(0, "v", bank_of("sum0"))
        transpose_h(1, "v", bank_of("sum1"))
        warm_up(4, bank_of("work3"))
        transpose_w1(0, "s", bank_of("sum2"))
        transpose_w1(1, "s", bank_of("sum3"))
        quantise_h(0)
        quantise_h(1)
        prepare_biases(new_bank())
        quantise_w1(0)
        transpose_w1(2, "v")
        quantise_w1(1)
        transpose_w1(3, "s")
        quantise_w1(2)
        quantise_w1(3)
        start_unit(0)
        s_route(0, (0, 1))
        transpose_w2(0, 0, "v", bank_of("sum0"))
        s_route(0, (2, 3))
        transpose_w2(0, 1, "v", bank_of("sum1"))
        transpose_w1(4, "s", bank_of("sum2"))
        transpose_w1(5, "s", bank_of("sum3"))
        quantise_w2(0)
        for u in (1, 2, 3):
            start_unit(u)
            s_route(u, (0, 1, 2, 3))
            if u >= 2:
                second_matmul(u - 2)
            if u == 3:
                quantise_h(2, 2)
            regroup(u - 1, 0, 512)
            if u < 3:
                quantise_w1(2 * u + 2, 2)
            spare = [bank_of("sum%d" % c) for c in range(4)] if u == 1 else [None] * 4
            transpose_w2(u, 0, "v", spare[0])
            transpose_w2(u, 1, "s", spare[1])
            if u + 2 < 4:
                if u == 1:
                    warm_up(4, spare[2])
                transpose_w1(2 * u + 4, "s", spare[2])
                transpose_w1(2 * u + 5, "s", spare[3])
            if u == 2:
                transpose_h(2, "s")
                transpose_h(3, "s")
            quantise_a(u - 1, 0, 512)
            quantise_w2(u)
        for u in (4, 5, 6, 7):
            start_unit(u)
            if u == 7:
                s_route(u, (0, 1, 2, 3), 0, 256)
                s_route(u, (0, 1, 2, 3), 256, 256)
            else:
                s_route(u, (0, 1, 2, 3))
            if u < 6:
                second_matmul(u - 2)
            regroup_unit(u - 1)
            if u == 6:
                for c in range(3):
                    add_residual(0, c, 0, 512, c)
            if u == 7:
                sums_of_second_half(4, range(3))
                sums_of_second_half(5, range(3))
            quantise_unit(u - 1)
        sums_of_second_half(6, range(3))
        nc.scalar.copy(
            out=a_grouped[7][:, 0:256, :].rearrange("p (c n) v -> p c v n", n=4),
            in_=a_rows[7][:, :, 0:256].rearrange("p v (c n) -> p c v n", n=4),
        )
        sum_squares(0, 0, 512, 0, 3)
        for u in (4, 5, 6):
            sums_of_second_half(u, (3,))
        regroup(7, 256, 256)
        quantise_a(7, 0, 256)
        quantise_a(7, 256, 256)
        sums_of_second_half(7, range(D_TILES))
        add_residual(0, 3, 0, 512, 3)
        sum_squares(3, 0, 512, 3)
        for c in range(D_TILES):
            add_residual(1, c, 512, 512, 4 + c)
            sum_squares(c, 512, 512, 4 + c)
        for i in range(3):
            transpose_back(i, "work%d" % (i + 1))
        transpose_back(3, "sum2")
        mean_ps = bank_of("sum0")
        nc.tensor.matmul(out=mean_ps[:, 0:COLS], lhsT=mean_w[:], rhs=partial[:, 0, :], start=True, stop=True)
        msq_ps = bank_of("sum1")
        nc.tensor.matmul(out=msq_ps[:, 0:COLS], lhsT=mean_w[:], rhs=partial[:, 1, :], start=True, stop=True)
        mean = keep.tile([P, 1], F32)
        nc.vector.tensor_reduce(out=mean[:], in_=mean_ps[:, 0:COLS], axis=AXIS.X, op=ALU.add)
        neg_mean = keep.tile([P, 1], F32)
        nc.vector.tensor_scalar(out=neg_mean[:], in0=mean[:], scalar1=-1.0, scalar2=None, op0=ALU.mult)
        eps_less = keep.tile([P, 1], F32)
        nc.vector.scalar_tensor_tensor(out=eps_less[:], in0=mean[:], scalar=neg_mean[:], in1=eps_col[:], op0=ALU.mult, op1=ALU.add)
        msq_cols = keep.tile([P, COLS], F32)
        msq = keep.tile([P, 1], F32)
        nc.scalar.activation(out=msq_cols[:], in_=msq_ps[:, 0:COLS], func=ACT.Copy, accum_out=msq[:])
        rstd = keep.tile([P, 1], F32)
        nc.scalar.activation(out=rstd[:], in_=msq[:], func=ACT.Abs_reciprocal_sqrt, scale=1.0, bias=eps_less[:])
        shift = keep.tile([P, 1], F32)
        nc.scalar.activation(out=shift[:], in_=rstd[:], func=ACT.Copy, scale=neg_mean[:])
        transpose_back(4, "work0")
        transpose_back(5, "sum3")
        transpose_back(6, "sum0")
        transpose_back(7, "sum1")
        for half in range(2):
            normalise(0, "v", half)
            nc.sync.dma_start(out=out_view[:, 0, half * 256 : (half + 1) * 256], in_=y_sb[:, 0, half * 256 : (half + 1) * 256])
        for i in range(1, TOKEN_TILES):
            normalise(i, "sv"[i % 2] if i > 1 else "s")
            if i == 1:
                nc.sync.dma_start(out=out_view[:, i, :], in_=y_sb[:, i, :])
            elif i % 2 == 1:
                nc.sync.dma_start(out=out_view[:, i - 1 : i + 1, :], in_=y_sb[:, i - 1 : i + 1, :])
